import numpy as np
import ml_dtypes


def mxq(x, axis, fmt="e4m3"):
    dtype, down = {"e4m3": (ml_dtypes.float8_e4m3fn, 7), "e5m2": (ml_dtypes.float8_e5m2, 14)}[fmt]
    v = np.moveaxis(np.asarray(x, np.float32).astype(ml_dtypes.bfloat16).astype(np.float64), axis, -1)
    blocks = v.reshape(v.shape[:-1] + (-1, 32))
    amax = np.abs(blocks).max(-1, keepdims=True)
    byte = np.maximum(np.where(amax > 0, np.frexp(amax)[1] - 1 + 127, 0) - down, 1)
    scale = np.exp2(byte - 127.0)
    codes = (blocks / scale).astype(np.float32).astype(dtype).astype(np.float64)
    return np.moveaxis((codes * scale).reshape(v.shape), -1, axis)


WIDE = False


def mx_kscale(k):
    if not WIDE:
        return np.ones(k)
    levels = np.array([10, -10, 5, -5, 0])
    if k % 512:
        return np.exp2(np.random.permutation(np.resize(levels, k // 32))).repeat(32)
    a = np.empty((k // 512, 16))
    for p in range(k // 512):
        a[p, :8] = np.random.permutation(np.resize(levels, 8))
        for g in range(8):
            far = levels[np.abs(levels - a[p, g]) >= 10]
            a[p, g + 8] = far[np.random.randint(len(far))]
    return np.exp2(a.ravel()).repeat(32)


BF16 = ml_dtypes.bfloat16


def bf(x):
    return np.asarray(x, np.float32).astype(BF16)


def f64(x):
    return np.asarray(x).astype(np.float64)


B, S, H, D = 8, 512, 2, 256


def setup_inputs():
    s = mx_kscale(S)
    bias = np.random.standard_normal((1, 1, S, S)) + np.log(s)
    shut = np.random.random((1, 1, S, S)) < 0.125
    return {"q": bf(np.random.standard_normal((B, S, H, D))),
            "k": bf(np.random.standard_normal((B, S, H, D))),
            "v": bf(np.random.standard_normal((B, S, H, D)) * (np.sqrt(S) / 8.0) * s.mean() / s[None, :, None, None]),
            "start_pos": 0, "seqlen": S,
            "mask": bf(np.where(shut, -1e9, bias))}


def reference(q, k, v, start_pos, seqlen, mask):
    qs = f64(q).transpose(0, 2, 1, 3)
    ks = f64(k).transpose(0, 2, 1, 3)
    vs = f64(v).transpose(0, 2, 1, 3)
    scores = qs @ ks.transpose(0, 1, 3, 2) / np.sqrt(D)
    scores = scores + f64(mask)
    e = np.exp(scores - scores.max(-1, keepdims=True))
    out = (mxq(e, 3, "e4m3") @ mxq(vs, 2, "e4m3")) / e.sum(-1, keepdims=True)
    return out.transpose(0, 2, 1, 3)

@@ -1,0 +1,350 @@
+from contextlib import ExitStack
+
+import concourse.bass as bass
+import concourse.mybir as mybir
+import concourse.tile as tile
+from concourse.masks import make_identity
+
+F32 = mybir.dt.float32
+BF16 = mybir.dt.bfloat16
+U32 = mybir.dt.uint32
+U8 = mybir.dt.uint8
+FP8X4 = mybir.dt.float8_e4m3fn_x4
+ALU = mybir.AluOpType
+ACTF = mybir.ActivationFunctionType
+AX = mybir.AxisListType
+
+B, S, H, D = 8, 512, 2, 256
+P = 128
+NT = S // P
+NS = B * NT
+FLOPS = 2 * (2 * B * H * S * S * D)
+
+MANUAL = True
+NLAST = 2
+E_REGROUP = "pool"
+V_REGROUP = "pool"
+
+
+def tile_attention_gear_t_kernel(tc, q, k, v, start_pos, seqlen, mask, out):
+    nc = tc.nc
+    with ExitStack() as ctx:
+        if MANUAL:
+            ctx.enter_context(tc.manual_schedule())
+        const = ctx.enter_context(tc.tile_pool(name="const", bufs=1))
+        raw = ctx.enter_context(tc.tile_pool(name="raw", bufs=2))
+        tp = ctx.enter_context(tc.tile_pool(name="tp", bufs=2))
+        work = ctx.enter_context(tc.tile_pool(name="work", bufs=2))
+        small = ctx.enter_context(tc.tile_pool(name="small", bufs=3))
+        ps_s = ctx.enter_context(tc.psum_pool(name="ps_s", bufs=4))
+        ps_t = ctx.enter_context(tc.psum_pool(name="ps_t", bufs=1))
+        ps_e = ctx.enter_context(tc.psum_pool(name="ps_e", bufs=2))
+        ps_o = ctx.enter_context(tc.psum_pool(name="ps_o", bufs=1))
+
+        st = {}
+
+        def load_kq(b):
+            k_raw = raw.tile([P, NT, H * D], BF16, tag="k_raw")
+            nc.sync.dma_start(out=k_raw[:], in_=k[b].rearrange("(p t) h d -> p t (h d)", t=NT))
+            q_raw = raw.tile([P, NT, H * D], BF16, tag="q_raw")
+            nc.sync.dma_start(out=q_raw[:], in_=q[b].rearrange("(p j) h d -> p j (h d)", j=NT))
+            st[("k_raw", b)] = k_raw
+            st[("q_raw", b)] = q_raw
+
+        def load_v(b):
+            v_raw = raw.tile([P, NT, H * D], BF16, tag="v_raw", bufs=3)
+            nc.sync.dma_start(out=v_raw[:], in_=v[b].rearrange("(p t) h d -> p t (h d)", t=NT))
+            st[("v_raw", b)] = v_raw
+
+        load_kq(0)
+        mask_raw = const.tile([P, NT, S], BF16, name="mask_raw")
+        nc.sync.dma_start(out=mask_raw[:], in_=mask[0, 0].rearrange("(p j) c -> p j c", j=NT))
+        load_kq(1)
+        load_v(0)
+        load_v(1)
+
+        ident_f = const.tile([P, P], F32, name="ident_f")
+        make_identity(nc, ident_f[:])
+        ident_b = const.tile([P, P], BF16, name="ident_b")
+        make_identity(nc, ident_b[:])
+        ident16 = const.tile([P, P], BF16, name="ident16")
+        nc.gpsimd.tensor_scalar(out=ident16[:], in0=ident_b[:], scalar1=16.0, scalar2=0.0, op0=ALU.mult, op1=ALU.add)
+        mask_sb = const.tile([P, NT, S], BF16, name="mask_sb")
+        for j in range(NT):
+            nc.vector.tensor_copy(
+                out=mask_sb[:, j, :].rearrange("p (t c) -> p t c", t=NT),
+                in_=mask_raw[:, j, :].rearrange("p (c t) -> p t c", t=NT),
+            )
+        warm = const.tile([P, 1], F32, name="warm")
+        nc.gpsimd.memset(warm[:], 0.0)
+        nc.scalar.activation(out=warm[:], in_=warm[:], func=ACTF.Exp)
+
+        def prep_t(b, r, pool, tag):
+            which = "k" if r < 2 else "q"
+            h = r % 2
+            src = st[(which + "_raw", b)]
+            pt = pool.tile([P, S], F32, tag=tag, name="pt")
+            words = src[:].bitcast(F32)
+            for i in range(NT):
+                nc.tensor.transpose(
+                    out=pt[:, i * P:(i + 1) * P],
+                    in_=words[:, i, h * P:(h + 1) * P],
+                    identity=ident_f[:],
+                )
+            st[("pt", b, r)] = pt
+
+        def prep_evac(b, r, eng):
+            which = "k" if r < 2 else "q"
+            h = r % 2
+            dst = tp.tile([P, S], F32, tag="%sT%d" % (which, h), name="dstT")
+            pt = st[("pt", b, r)]
+            if eng == "act":
+                nc.scalar.copy(out=dst[:], in_=pt[:])
+            else:
+                nc.vector.tensor_copy(out=dst[:], in_=pt[:])
+            st[(which + "T", b, h)] = dst[:].bitcast(BF16).rearrange("p (s e) -> p s e", e=2)
+
+        def pe_mask(n, hh):
+            return hh == 0 and (3 * n) % 8 < 3
+
+        def qk(n, hh):
+            b, j = divmod(n, NT)
+            ps = ps_s.tile([P, S], F32, tag="s", name="ps")
+            qT = st[("qT", b, hh)]
+            kT = st[("kT", b, hh)]
+            on_pe = pe_mask(n, hh)
+            for e in range(2):
+                nc.tensor.matmul(
+                    out=ps[:],
+                    lhsT=qT[:, j * P:(j + 1) * P, e],
+                    rhs=kT[:, :, e],
+                    start=(e == 0),
+                    stop=(e == 1 and not on_pe),
+                )
+            if on_pe:
+                nc.tensor.matmul(out=ps[:], lhsT=ident16[:], rhs=mask_sb[:, j, :], start=False, stop=True)
+            st[("ps", n, hh)] = ps
+
+        def stt(n, hh):
+            b, j = divmod(n, NT)
+            if hh == 0:
+                st[("s2", n)] = work.tile([P, H, S], F32, tag="s2", name="s2", bufs=3)
+                st[("negm", n)] = small.tile([P, H], F32, tag="negm", name="negm")
+            s2 = st[("s2", n)]
+            if pe_mask(n, hh):
+                nc.vector.tensor_scalar(
+                    out=s2[:, hh, :],
+                    in0=st[("ps", n, hh)][:],
+                    scalar1=-1.0 / 16.0,
+                    scalar2=None,
+                    op0=ALU.mult,
+                    op1=ALU.min,
+                    accum_out=st[("negm", n)][:, hh:hh + 1],
+                )
+                return
+            nc.vector.scalar_tensor_tensor(
+                out=s2[:, hh, :],
+                in0=st[("ps", n, hh)][:],
+                scalar=-1.0 / 16.0,
+                in1=mask_sb[:, j, :],
+                op0=ALU.mult,
+                op1=ALU.subtract,
+            )
+
+        def rowmin(n):
+            negm = st[("negm", n)]
+            if pe_mask(n, 0):
+                nc.vector.tensor_reduce(out=negm[:, 1:2], in_=st[("s2", n)][:, 1, :], axis=AX.X, op=ALU.min)
+            else:
+                nc.vector.tensor_reduce(out=negm[:], in_=st[("s2", n)][:], axis=AX.X, op=ALU.min)
+
+        def expo(n, hh):
+            if hh == 0:
+                st[("e2", n)] = work.tile([P, H, S], BF16, tag="e2", name="e2")
+                st[("rs", n)] = small.tile([P, H], F32, tag="rs", name="rs", bufs=5)
+            nc.scalar.activation(
+                out=st[("e2", n)][:, hh, :],
+                in_=st[("s2", n)][:, hh, :],
+                func=ACTF.Exp,
+                bias=st[("negm", n)][:, hh:hh + 1],
+                scale=-1.0,
+                accum_out=st[("rs", n)][:, hh:hh + 1],
+            )
+
+        def e_t(n, hh):
+            if hh == 0:
+                st[("pe", n)] = ps_e.tile([P, NT, H, P], BF16, tag="pe", name="pe")
+            pe = st[("pe", n)]
+            e2 = st[("e2", n)]
+            for t in range(NT):
+                nc.tensor.transpose(
+                    out=pe[:, t, hh, :],
+                    in_=e2[:, hh, t * P:(t + 1) * P],
+                    identity=ident_b[:],
+                )
+
+        def evac_t(n):
+            epl = work.tile([P, NT, H * P], BF16, tag="epl", name="epl")
+            nc.scalar.copy(
+                out=epl[:].rearrange("p t c -> p (t c)"),
+                in_=st[("pe", n)][:].rearrange("p t h c -> p (t h c)"),
+            )
+            st[("epl", n)] = epl
+
+        def regroup(dst, src, eng):
+            if eng == "pool":
+                nc.gpsimd.tensor_scalar(
+                    out=dst,
+                    in0=src.rearrange("p t c -> p c t"),
+                    scalar1=1.0,
+                    scalar2=0.0,
+                    op0=ALU.mult,
+                    op1=ALU.add,
+                )
+            else:
+                nc.vector.tensor_copy(
+                    out=dst.rearrange("p (c i) t -> p c t i", i=4),
+                    in_=src.rearrange("p t (c i) -> p c t i", i=4),
+                )
+
+        def regroup_e(n):
+            grp = work.tile([P, H * P, NT], BF16, tag="grp", name="grp", bufs=3, align_bytes=64)
+            regroup(grp[:], st[("epl", n)][:], E_REGROUP)
+            st[("grp", n)] = grp
+
+        def evac_regroup_e(n):
+            grp = work.tile([P, H * P, NT], BF16, tag="grp", name="grp", bufs=3, align_bytes=64)
+            nc.vector.tensor_copy(out=grp[:], in_=st[("pe", n)][:].rearrange("p t h c -> p (h c) t"))
+            st[("grp", n)] = grp
+
+        def quant_e(n):
+            ec = work.tile([P, H * P], U32, tag="ec", name="ec", align_bytes=64)
+            es = work.tile([P, H * P], U8, tag="es", name="es", align_bytes=64)
+            nc.vector.quantize_mx(
+                out=ec[:].bitcast(FP8X4),
+                scales=es[:],
+                in_=st[("grp", n)][:].rearrange("p c t -> p (c t)"),
+            )
+            rc = small.tile([P, H], F32, tag="rc", name="rc")
+            nc.vector.reciprocal(out=rc[:], in_=st[("rs", n)][:])
+            st[("ec", n)] = ec
+            st[("es", n)] = es
+            st[("rc", n)] = rc
+
+        def regroup_v(b, r):
+            if r == 0:
+                st[("vgrp", b)] = work.tile([P, H * D, NT], BF16, tag="vgrp", name="vgrp", align_bytes=64)
+            cs = slice(r * P, (r + 1) * P)
+            regroup(st[("vgrp", b)][:, cs, :], st[("v_raw", b)][:, :, cs], V_REGROUP)
+
+        def quant_v(b):
+            vc = work.tile([P, H * D], U32, tag="vc", name="vc", align_bytes=64)
+            vs = work.tile([P, H * D], U8, tag="vs", name="vs", align_bytes=64)
+            nc.vector.quantize_mx(
+                out=vc[:].bitcast(FP8X4),
+                scales=vs[:],
+                in_=st[("vgrp", b)][:].rearrange("p c t -> p (c t)"),
+            )
+            st[("vc", b)] = vc
+            st[("vs", b)] = vs
+
+        def pv(n):
+            b, j = divmod(n, NT)
+            if n >= NS - NLAST:
+                po = ps_s.tile([P, H, D], F32, tag="s", name="po")
+            else:
+                po = ps_o.tile([P, H, D], F32, tag="po", name="po")
+            for hh in range(H):
+                nc.tensor.matmul_mx(
+                    out=po[:, hh, :],
+                    lhsT=st[("ec", n)][:, hh * P:(hh + 1) * P].bitcast(FP8X4),
+                    lhsT_scale=st[("es", n)][:, hh * P:(hh + 1) * P],
+                    rhs=st[("vc", b)][:, hh * D:(hh + 1) * D].bitcast(FP8X4),
+                    rhs_scale=st[("vs", b)][:, hh * D:(hh + 1) * D],
+                    start=True,
+                    stop=True,
+                )
+            st[("po", n)] = po
+
+        def o_evac(n):
+            ob = work.tile([P, H, D], F32, tag="ob", name="ob", bufs=4)
+            for hh in range(H):
+                nc.scalar.activation(
+                    out=ob[:, hh, :],
+                    in_=st[("po", n)][:, hh, :],
+                    func=ACTF.Copy,
+                    scale=st[("rc", n)][:, hh:hh + 1],
+                )
+            st[("ob", n)] = ob
+
+        def store(n):
+            b, j = divmod(n, NT)
+            nc.sync.dma_start(
+                out=out[b].rearrange("(p j) h d -> p j (h d)", j=NT)[:, j, :],
+                in_=st[("ob", n)][:].rearrange("p h d -> p (h d)"),
+            )
+
+        for r in range(4):
+            prep_t(0, r, ps_s, "s")
+        for r in range(4):
+            prep_evac(0, r, "act" if r % 2 == 0 else "dve")
+
+        def ok(n):
+            return 0 <= n < NS
+
+        def preps(c):
+            if c in (0, 1):
+                return [(1, 2 * c), (1, 2 * c + 1)]
+            x = c + 2
+            b1 = x // 4 + 1
+            if c >= 2 and b1 < B:
+                return [(b1, x % 4)]
+            return []
+
+        LAG = 3
+        for c in range(-2, NS + LAG):
+            pl = preps(c)
+            for i, u in enumerate(pl):
+                if i == 0:
+                    prep_t(u[0], u[1], ps_t, "t")
+                else:
+                    prep_t(u[0], u[1], ps_o, "po")
+            if ok(c + 2):
+                qk(c + 2, 0)
+            if ok(c + 1):
+                stt(c + 1, 0)
+            if ok(c - LAG):
+                if (c - LAG) % NT == 0:
+                    quant_v((c - LAG) // NT)
+                quant_e(c - LAG)
+                pv(c - LAG)
+            if ok(c):
+                expo(c, 0)
+                e_t(c, 0)
+            if ok(c - 1):
+                if c - 1 >= NS - NLAST:
+                    evac_regroup_e(c - 1)
+                else:
+                    evac_t(c - 1)
+                    regroup_e(c - 1)
+            xb, xr = divmod(c + 2, NT)
+            if xb < B:
+                regroup_v(xb, xr)
+            if ok(c + 2):
+                qk(c + 2, 1)
+            if ok(c + 1):
+                stt(c + 1, 1)
+                rowmin(c + 1)
+            if ok(c):
+                expo(c, 1)
+                e_t(c, 1)
+            for u in pl:
+                prep_evac(u[0], u[1], "act")
+            if ok(c - LAG):
+                o_evac(c - LAG)
+                store(c - LAG)
+            if (c + 2) % NT == 0:
+                nb = (c + 2) // NT + 2
+                if nb < B:
+                    load_kq(nb)
+                    load_v(nb)

@@ -20,17 +20,13 @@ NT = S // P
 NS = B * NT
 FLOPS = 2 * (2 * B * H * S * S * D)
 
-MANUAL = True
-NLAST = 2
-E_REGROUP = "pool"
-V_REGROUP = "pool"
+U = 2
 
 
 def tile_attention_gear_t_kernel(tc, q, k, v, start_pos, seqlen, mask, out):
     nc = tc.nc
     with ExitStack() as ctx:
-        if MANUAL:
-            ctx.enter_context(tc.manual_schedule())
+        ctx.enter_context(tc.manual_schedule())
         const = ctx.enter_context(tc.tile_pool(name="const", bufs=1))
         raw = ctx.enter_context(tc.tile_pool(name="raw", bufs=2))
         tp = ctx.enter_context(tc.tile_pool(name="tp", bufs=2))
@@ -45,7 +41,7 @@ def tile_attention_gear_t_kernel(tc, q, k, v, start_pos, seqlen, mask, out):
 
         def load_kq(b):
             k_raw = raw.tile([P, NT, H * D], BF16, tag="k_raw")
-            nc.sync.dma_start(out=k_raw[:], in_=k[b].rearrange("(p t) h d -> p t (h d)", t=NT))
+            nc.sync.dma_start(out=k_raw[:], in_=k[b].rearrange("(t p) h d -> p t (h d)", p=P))
             q_raw = raw.tile([P, NT, H * D], BF16, tag="q_raw")
             nc.sync.dma_start(out=q_raw[:], in_=q[b].rearrange("(p j) h d -> p j (h d)", j=NT))
             st[("k_raw", b)] = k_raw
@@ -57,8 +53,8 @@ def tile_attention_gear_t_kernel(tc, q, k, v, start_pos, seqlen, mask, out):
             st[("v_raw", b)] = v_raw
 
         load_kq(0)
-        mask_raw = const.tile([P, NT, S], BF16, name="mask_raw")
-        nc.sync.dma_start(out=mask_raw[:], in_=mask[0, 0].rearrange("(p j) c -> p j c", j=NT))
+        mask_sb = const.tile([P, NT, S], BF16, name="mask_sb")
+        nc.sync.dma_start(out=mask_sb[:], in_=mask[0, 0].rearrange("(p j) c -> p j c", j=NT))
         load_kq(1)
         load_v(0)
         load_v(1)
@@ -69,12 +65,6 @@ def tile_attention_gear_t_kernel(tc, q, k, v, start_pos, seqlen, mask, out):
         make_identity(nc, ident_b[:])
         ident16 = const.tile([P, P], BF16, name="ident16")
         nc.gpsimd.tensor_scalar(out=ident16[:], in0=ident_b[:], scalar1=16.0, scalar2=0.0, op0=ALU.mult, op1=ALU.add)
-        mask_sb = const.tile([P, NT, S], BF16, name="mask_sb")
-        for j in range(NT):
-            nc.vector.tensor_copy(
-                out=mask_sb[:, j, :].rearrange("p (t c) -> p t c", t=NT),
-                in_=mask_raw[:, j, :].rearrange("p (c t) -> p t c", t=NT),
-            )
         warm = const.tile([P, 1], F32, name="warm")
         nc.gpsimd.memset(warm[:], 0.0)
         nc.scalar.activation(out=warm[:], in_=warm[:], func=ACTF.Exp)
@@ -151,20 +141,20 @@ def tile_attention_gear_t_kernel(tc, q, k, v, start_pos, seqlen, mask, out):
                 op1=ALU.subtract,
             )
 
-        def rowmin(n):
-            negm = st[("negm", n)]
-            if pe_mask(n, 0):
-                nc.vector.tensor_reduce(out=negm[:, 1:2], in_=st[("s2", n)][:, 1, :], axis=AX.X, op=ALU.min)
-            else:
-                nc.vector.tensor_reduce(out=negm[:], in_=st[("s2", n)][:], axis=AX.X, op=ALU.min)
+        def rowmin(n, hh):
+            if pe_mask(n, hh):
+                return
+            nc.vector.tensor_reduce(
+                out=st[("negm", n)][:, hh:hh + 1], in_=st[("s2", n)][:, hh, :], axis=AX.X, op=ALU.min
+            )
 
         def expo(n, hh):
             if hh == 0:
                 st[("e2", n)] = work.tile([P, H, S], BF16, tag="e2", name="e2")
                 st[("rs", n)] = small.tile([P, H], F32, tag="rs", name="rs", bufs=5)
             nc.scalar.activation(
-                out=st[("e2", n)][:, hh, :],
-                in_=st[("s2", n)][:, hh, :],
+                out=st[("e2", n)][:, hh, :].rearrange("p (u w e) -> p u w e", u=U, e=2),
+                in_=st[("s2", n)][:, hh, :].rearrange("p (w u e) -> p u w e", u=U, e=2),
                 func=ACTF.Exp,
                 bias=st[("negm", n)][:, hh:hh + 1],
                 scale=-1.0,
@@ -173,48 +163,22 @@ def tile_attention_gear_t_kernel(tc, q, k, v, start_pos, seqlen, mask, out):
 
         def e_t(n, hh):
             if hh == 0:
-                st[("pe", n)] = ps_e.tile([P, NT, H, P], BF16, tag="pe", name="pe")
+                st[("pe", n)] = ps_e.tile([P, U, H, P], F32, tag="pe", name="pe")
             pe = st[("pe", n)]
-            e2 = st[("e2", n)]
-            for t in range(NT):
+            words = st[("e2", n)][:].bitcast(F32)
+            for u in range(U):
                 nc.tensor.transpose(
-                    out=pe[:, t, hh, :],
-                    in_=e2[:, hh, t * P:(t + 1) * P],
-                    identity=ident_b[:],
+                    out=pe[:, u, hh, :],
+                    in_=words[:, hh, u * P:(u + 1) * P],
+                    identity=ident_f[:],
                 )
 
-        def evac_t(n):
-            epl = work.tile([P, NT, H * P], BF16, tag="epl", name="epl")
+        def evac_e(n):
+            grp = work.tile([P, H * P, NT], BF16, tag="grp", name="grp", bufs=3, align_bytes=64)
             nc.scalar.copy(
-                out=epl[:].rearrange("p t c -> p (t c)"),
-                in_=st[("pe", n)][:].rearrange("p t h c -> p (t h c)"),
+                out=grp[:].bitcast(F32),
+                in_=st[("pe", n)][:].rearrange("p u h c -> p (h c) u"),
             )
-            st[("epl", n)] = epl
-
-        def regroup(dst, src, eng):
-            if eng == "pool":
-                nc.gpsimd.tensor_scalar(
-                    out=dst,
-                    in0=src.rearrange("p t c -> p c t"),
-                    scalar1=1.0,
-                    scalar2=0.0,
-                    op0=ALU.mult,
-                    op1=ALU.add,
-                )
-            else:
-                nc.vector.tensor_copy(
-                    out=dst.rearrange("p (c i) t -> p c t i", i=4),
-                    in_=src.rearrange("p t (c i) -> p c t i", i=4),
-                )
-
-        def regroup_e(n):
-            grp = work.tile([P, H * P, NT], BF16, tag="grp", name="grp", bufs=3, align_bytes=64)
-            regroup(grp[:], st[("epl", n)][:], E_REGROUP)
-            st[("grp", n)] = grp
-
-        def evac_regroup_e(n):
-            grp = work.tile([P, H * P, NT], BF16, tag="grp", name="grp", bufs=3, align_bytes=64)
-            nc.vector.tensor_copy(out=grp[:], in_=st[("pe", n)][:].rearrange("p t h c -> p (h c) t"))
             st[("grp", n)] = grp
 
         def quant_e(n):
@@ -225,17 +189,26 @@ def tile_attention_gear_t_kernel(tc, q, k, v, start_pos, seqlen, mask, out):
                 scales=es[:],
                 in_=st[("grp", n)][:].rearrange("p c t -> p (c t)"),
             )
-            rc = small.tile([P, H], F32, tag="rc", name="rc")
-            nc.vector.reciprocal(out=rc[:], in_=st[("rs", n)][:])
             st[("ec", n)] = ec
             st[("es", n)] = es
+
+        def recip(n):
+            rc = small.tile([P, H], F32, tag="rc", name="rc")
+            nc.vector.reciprocal(out=rc[:], in_=st[("rs", n)][:])
             st[("rc", n)] = rc
 
         def regroup_v(b, r):
             if r == 0:
                 st[("vgrp", b)] = work.tile([P, H * D, NT], BF16, tag="vgrp", name="vgrp", align_bytes=64)
             cs = slice(r * P, (r + 1) * P)
-            regroup(st[("vgrp", b)][:, cs, :], st[("v_raw", b)][:, :, cs], V_REGROUP)
+            nc.gpsimd.tensor_scalar(
+                out=st[("vgrp", b)][:, cs, :],
+                in0=st[("v_raw", b)][:, :, cs].rearrange("p t c -> p c t"),
+                scalar1=1.0,
+                scalar2=0.0,
+                op0=ALU.mult,
+                op1=ALU.add,
+            )
 
         def quant_v(b):
             vc = work.tile([P, H * D], U32, tag="vc", name="vc", align_bytes=64)
@@ -250,10 +223,7 @@ def tile_attention_gear_t_kernel(tc, q, k, v, start_pos, seqlen, mask, out):
 
         def pv(n):
             b, j = divmod(n, NT)
-            if n >= NS - NLAST:
-                po = ps_s.tile([P, H, D], F32, tag="s", name="po")
-            else:
-                po = ps_o.tile([P, H, D], F32, tag="po", name="po")
+            po = ps_o.tile([P, H, D], F32, tag="po", name="po")
             for hh in range(H):
                 nc.tensor.matmul_mx(
                     out=po[:, hh, :],
@@ -301,7 +271,7 @@ def tile_attention_gear_t_kernel(tc, q, k, v, start_pos, seqlen, mask, out):
                 return [(b1, x % 4)]
             return []
 
-        LAG = 3
+        LAG = 2
         for c in range(-2, NS + LAG):
             pl = preps(c)
             for i, u in enumerate(pl):
@@ -322,11 +292,7 @@ def tile_attention_gear_t_kernel(tc, q, k, v, start_pos, seqlen, mask, out):
                 expo(c, 0)
                 e_t(c, 0)
             if ok(c - 1):
-                if c - 1 >= NS - NLAST:
-                    evac_regroup_e(c - 1)
-                else:
-                    evac_t(c - 1)
-                    regroup_e(c - 1)
+                evac_e(c - 1)
             xb, xr = divmod(c + 2, NT)
             if xb < B:
                 regroup_v(xb, xr)
@@ -334,15 +300,19 @@ def tile_attention_gear_t_kernel(tc, q, k, v, start_pos, seqlen, mask, out):
                 qk(c + 2, 1)
             if ok(c + 1):
                 stt(c + 1, 1)
-                rowmin(c + 1)
+                rowmin(c + 1, 0)
+            if ok(c - LAG):
+                recip(c - LAG)
+            if ok(c + 1):
+                rowmin(c + 1, 1)
             if ok(c):
                 expo(c, 1)
                 e_t(c, 1)
-            for u in pl:
-                prep_evac(u[0], u[1], "act")
             if ok(c - LAG):
                 o_evac(c - LAG)
                 store(c - LAG)
+            for u in pl:
+                prep_evac(u[0], u[1], "act")
             if (c + 2) % NT == 0:
                 nb = (c + 2) // NT + 2
                 if nb < B:

@@ -1,8 +1,6 @@
 from contextlib import ExitStack
 
-import concourse.bass as bass
 import concourse.mybir as mybir
-import concourse.tile as tile
 from concourse.masks import make_identity
 
 F32 = mybir.dt.float32
@@ -20,6 +18,7 @@ NT = S // P
 NS = B * NT
 FLOPS = 2 * (2 * B * H * S * S * D)
 
+NMM = 12
 U = 2
 
 
@@ -30,14 +29,17 @@ def tile_attention_gear_t_kernel(tc, q, k, v, start_pos, seqlen, mask, out):
         const = ctx.enter_context(tc.tile_pool(name="const", bufs=1))
         raw = ctx.enter_context(tc.tile_pool(name="raw", bufs=2))
         tp = ctx.enter_context(tc.tile_pool(name="tp", bufs=2))
-        work = ctx.enter_context(tc.tile_pool(name="work", bufs=2))
-        small = ctx.enter_context(tc.tile_pool(name="small", bufs=3))
+        work = ctx.enter_context(tc.tile_pool(name="work", bufs=3))
+        small = ctx.enter_context(tc.tile_pool(name="small", bufs=4))
         ps_s = ctx.enter_context(tc.psum_pool(name="ps_s", bufs=4))
         ps_t = ctx.enter_context(tc.psum_pool(name="ps_t", bufs=1))
-        ps_e = ctx.enter_context(tc.psum_pool(name="ps_e", bufs=2))
-        ps_o = ctx.enter_context(tc.psum_pool(name="ps_o", bufs=1))
+        ps_e = ctx.enter_context(tc.psum_pool(name="ps_e", bufs=1))
+        ps_o = ctx.enter_context(tc.psum_pool(name="ps_o", bufs=2))
 
         st = {}
+
+        def ok(n):
+            return 0 <= n < NS
 
         def load_kq(b):
             k_raw = raw.tile([P, NT, H * D], BF16, tag="k_raw")
@@ -48,7 +50,7 @@ def tile_attention_gear_t_kernel(tc, q, k, v, start_pos, seqlen, mask, out):
             st[("q_raw", b)] = q_raw
 
         def load_v(b):
-            v_raw = raw.tile([P, NT, H * D], BF16, tag="v_raw", bufs=3)
+            v_raw = raw.tile([P, NT, H * D], BF16, tag="v_raw", bufs=4)
             nc.sync.dma_start(out=v_raw[:], in_=v[b].rearrange("(p t) h d -> p t (h d)", t=NT))
             st[("v_raw", b)] = v_raw
 
@@ -68,13 +70,14 @@ def tile_attention_gear_t_kernel(tc, q, k, v, start_pos, seqlen, mask, out):
         warm = const.tile([P, 1], F32, name="warm")
         nc.gpsimd.memset(warm[:], 0.0)
         nc.scalar.activation(out=warm[:], in_=warm[:], func=ACTF.Exp)
+        maskT = const.tile([P, NT, NT, P], F32, name="maskT")
+
+        UNITS = [("k", 0), ("q", 0), ("k", 1), ("q", 1)]
 
         def prep_t(b, r, pool, tag):
-            which = "k" if r < 2 else "q"
-            h = r % 2
-            src = st[(which + "_raw", b)]
+            which, h = UNITS[r]
             pt = pool.tile([P, S], F32, tag=tag, name="pt")
-            words = src[:].bitcast(F32)
+            words = st[(which + "_raw", b)][:].bitcast(F32)
             for i in range(NT):
                 nc.tensor.transpose(
                     out=pt[:, i * P:(i + 1) * P],
@@ -84,8 +87,7 @@ def tile_attention_gear_t_kernel(tc, q, k, v, start_pos, seqlen, mask, out):
             st[("pt", b, r)] = pt
 
         def prep_evac(b, r, eng):
-            which = "k" if r < 2 else "q"
-            h = r % 2
+            which, h = UNITS[r]
             dst = tp.tile([P, S], F32, tag="%sT%d" % (which, h), name="dstT")
             pt = st[("pt", b, r)]
             if eng == "act":
@@ -94,64 +96,80 @@ def tile_attention_gear_t_kernel(tc, q, k, v, start_pos, seqlen, mask, out):
                 nc.vector.tensor_copy(out=dst[:], in_=pt[:])
             st[(which + "T", b, h)] = dst[:].bitcast(BF16).rearrange("p (s e) -> p s e", e=2)
 
-        def pe_mask(n, hh):
-            return hh == 0 and (3 * n) % 8 < 3
+        def maskT_t(j):
+            pm = ps_o.tile([P, NT, P], BF16, tag="po", name="pm")
+            for t in range(NT):
+                nc.tensor.transpose(out=pm[:, t, :], in_=mask_sb[:, j, t * P:(t + 1) * P], identity=ident_b[:])
+            st[("pm", j)] = pm
+
+        def maskT_evac(j):
+            nc.scalar.activation(out=maskT[:, j, :, :], in_=st[("pm", j)][:], func=ACTF.Copy, scale=16.0)
 
         def qk(n, hh):
             b, j = divmod(n, NT)
             ps = ps_s.tile([P, S], F32, tag="s", name="ps")
             qT = st[("qT", b, hh)]
             kT = st[("kT", b, hh)]
-            on_pe = pe_mask(n, hh)
             for e in range(2):
                 nc.tensor.matmul(
                     out=ps[:],
                     lhsT=qT[:, j * P:(j + 1) * P, e],
                     rhs=kT[:, :, e],
                     start=(e == 0),
-                    stop=(e == 1 and not on_pe),
+                    stop=(e == 1 and hh == 1),
                 )
-            if on_pe:
+            if hh == 0 and n < NMM:
                 nc.tensor.matmul(out=ps[:], lhsT=ident16[:], rhs=mask_sb[:, j, :], start=False, stop=True)
             st[("ps", n, hh)] = ps
 
-        def stt(n, hh):
+        def add_mask(n):
+            if n < NMM:
+                return
+            b, j = divmod(n, NT)
+            ps = st[("ps", n, 0)]
+            for t in range(NT):
+                nc.tensor.matmul(
+                    out=ps[:, t * P:(t + 1) * P],
+                    lhsT=maskT[:, j, t, :],
+                    rhs=ident_f[:],
+                    is_transpose=True,
+                    start=False,
+                    stop=(t == NT - 1),
+                )
+
+        def score(n, hh):
             b, j = divmod(n, NT)
             if hh == 0:
-                st[("s2", n)] = work.tile([P, H, S], F32, tag="s2", name="s2", bufs=3)
+                st[("s2", n)] = work.tile([P, H, S], F32, tag="s2", name="s2")
                 st[("negm", n)] = small.tile([P, H], F32, tag="negm", name="negm")
-            s2 = st[("s2", n)]
-            if pe_mask(n, hh):
                 nc.vector.tensor_scalar(
-                    out=s2[:, hh, :],
-                    in0=st[("ps", n, hh)][:],
+                    out=st[("s2", n)][:, 0, :],
+                    in0=st[("ps", n, 0)][:],
                     scalar1=-1.0 / 16.0,
                     scalar2=None,
                     op0=ALU.mult,
                     op1=ALU.min,
-                    accum_out=st[("negm", n)][:, hh:hh + 1],
+                    accum_out=st[("negm", n)][:, 0:1],
                 )
-                return
-            nc.vector.scalar_tensor_tensor(
-                out=s2[:, hh, :],
-                in0=st[("ps", n, hh)][:],
-                scalar=-1.0 / 16.0,
-                in1=mask_sb[:, j, :],
-                op0=ALU.mult,
-                op1=ALU.subtract,
-            )
+            else:
+                nc.vector.scalar_tensor_tensor(
+                    out=st[("s2", n)][:, 1, :],
+                    in0=st[("ps", n, 1)][:],
+                    scalar=-1.0 / 16.0,
+                    in1=mask_sb[:, j, :],
+                    op0=ALU.mult,
+                    op1=ALU.subtract,
+                )
 
-        def rowmin(n, hh):
-            if pe_mask(n, hh):
-                return
+        def rowmin1(n):
             nc.vector.tensor_reduce(
-                out=st[("negm", n)][:, hh:hh + 1], in_=st[("s2", n)][:, hh, :], axis=AX.X, op=ALU.min
+                out=st[("negm", n)][:, 1:2], in_=st[("s2", n)][:, 1, :], axis=AX.X, op=ALU.min
             )
 
         def expo(n, hh):
             if hh == 0:
                 st[("e2", n)] = work.tile([P, H, S], BF16, tag="e2", name="e2")
-                st[("rs", n)] = small.tile([P, H], F32, tag="rs", name="rs", bufs=5)
+                st[("rs", n)] = small.tile([P, H], F32, tag="rs", name="rs", bufs=6)
             nc.scalar.activation(
                 out=st[("e2", n)][:, hh, :].rearrange("p (u w e) -> p u w e", u=U, e=2),
                 in_=st[("s2", n)][:, hh, :].rearrange("p (w u e) -> p u w e", u=U, e=2),
@@ -161,20 +179,20 @@ def tile_attention_gear_t_kernel(tc, q, k, v, start_pos, seqlen, mask, out):
                 accum_out=st[("rs", n)][:, hh:hh + 1],
             )
 
-        def e_t(n, hh):
-            if hh == 0:
-                st[("pe", n)] = ps_e.tile([P, U, H, P], F32, tag="pe", name="pe")
-            pe = st[("pe", n)]
+        def e_t(n):
+            pe = ps_e.tile([P, U, H, P], F32, tag="pe", name="pe")
             words = st[("e2", n)][:].bitcast(F32)
-            for u in range(U):
-                nc.tensor.transpose(
-                    out=pe[:, u, hh, :],
-                    in_=words[:, hh, u * P:(u + 1) * P],
-                    identity=ident_f[:],
-                )
+            for hh in range(H):
+                for u in range(U):
+                    nc.tensor.transpose(
+                        out=pe[:, u, hh, :],
+                        in_=words[:, hh, u * P:(u + 1) * P],
+                        identity=ident_f[:],
+                    )
+            st[("pe", n)] = pe
 
         def evac_e(n):
-            grp = work.tile([P, H * P, NT], BF16, tag="grp", name="grp", bufs=3, align_bytes=64)
+            grp = work.tile([P, H * P, NT], BF16, tag="grp", name="grp", align_bytes=64)
             nc.scalar.copy(
                 out=grp[:].bitcast(F32),
                 in_=st[("pe", n)][:].rearrange("p u h c -> p (h c) u"),
@@ -199,7 +217,7 @@ def tile_attention_gear_t_kernel(tc, q, k, v, start_pos, seqlen, mask, out):
 
         def regroup_v(b, r):
             if r == 0:
-                st[("vgrp", b)] = work.tile([P, H * D, NT], BF16, tag="vgrp", name="vgrp", align_bytes=64)
+                st[("vgrp", b)] = work.tile([P, H * D, NT], BF16, tag="vgrp", name="vgrp", bufs=2, align_bytes=64)
             cs = slice(r * P, (r + 1) * P)
             nc.gpsimd.tensor_scalar(
                 out=st[("vgrp", b)][:, cs, :],
@@ -210,16 +228,16 @@ def tile_attention_gear_t_kernel(tc, q, k, v, start_pos, seqlen, mask, out):
                 op1=ALU.add,
             )
 
-        def quant_v(b):
-            vc = work.tile([P, H * D], U32, tag="vc", name="vc", align_bytes=64)
-            vs = work.tile([P, H * D], U8, tag="vs", name="vs", align_bytes=64)
+        def quant_v(b, r):
+            if r == 0:
+                st[("vc", b)] = work.tile([P, H * D], U32, tag="vc", name="vc", align_bytes=64)
+                st[("vs", b)] = work.tile([P, H * D], U8, tag="vs", name="vs", align_bytes=64)
+            cs = slice(r * P, (r + 1) * P)
             nc.vector.quantize_mx(
-                out=vc[:].bitcast(FP8X4),
-                scales=vs[:],
-                in_=st[("vgrp", b)][:].rearrange("p c t -> p (c t)"),
+                out=st[("vc", b)][:, cs].bitcast(FP8X4),
+                scales=st[("vs", b)][:, cs],
+                in_=st[("vgrp", b)][:, cs, :].rearrange("p c t -> p (c t)"),
             )
-            st[("vc", b)] = vc
-            st[("vs", b)] = vs
 
         def pv(n):
             b, j = divmod(n, NT)
@@ -238,6 +256,15 @@ def tile_attention_gear_t_kernel(tc, q, k, v, start_pos, seqlen, mask, out):
 
         def o_evac(n):
             ob = work.tile([P, H, D], F32, tag="ob", name="ob", bufs=4)
+            st[("ob", n)] = ob
+            if n % 2 == 1:
+                nc.vector.tensor_tensor(
+                    out=ob[:],
+                    in0=st[("po", n)][:],
+                    in1=st[("rc", n)][:].unsqueeze(2).to_broadcast([P, H, D]),
+                    op=ALU.mult,
+                )
+                return
             for hh in range(H):
                 nc.scalar.activation(
                     out=ob[:, hh, :],
@@ -245,7 +272,6 @@ def tile_attention_gear_t_kernel(tc, q, k, v, start_pos, seqlen, mask, out):
                     func=ACTF.Copy,
                     scale=st[("rc", n)][:, hh:hh + 1],
                 )
-            st[("ob", n)] = ob
 
         def store(n):
             b, j = divmod(n, NT)
@@ -259,62 +285,65 @@ def tile_attention_gear_t_kernel(tc, q, k, v, start_pos, seqlen, mask, out):
         for r in range(4):
             prep_evac(0, r, "act" if r % 2 == 0 else "dve")
 
-        def ok(n):
-            return 0 <= n < NS
-
         def preps(c):
-            if c in (0, 1):
-                return [(1, 2 * c), (1, 2 * c + 1)]
-            x = c + 2
-            b1 = x // 4 + 1
-            if c >= 2 and b1 < B:
-                return [(b1, x % 4)]
+            if c in (-1, 0):
+                return [(1, 2 * (c + 1)), (1, 2 * (c + 1) + 1)]
+            b1, r = divmod(c + 7, 4)
+            if c >= 1 and b1 < B:
+                return [(b1, r)]
             return []
 
-        LAG = 2
-        for c in range(-2, NS + LAG):
-            pl = preps(c)
-            for i, u in enumerate(pl):
+        MASKS = {1: [0], 2: [1], 3: [2, 3]}
+
+        for c in range(-2, NS + 5):
+            if ok(c + 2):
+                qk(c + 2, 0)
+            if ok(c - 4):
+                pv(c - 4)
+            if ok(c + 2):
+                qk(c + 2, 1)
+                add_mask(c + 2)
+            for i, u in enumerate(preps(c)):
                 if i == 0:
                     prep_t(u[0], u[1], ps_t, "t")
                 else:
                     prep_t(u[0], u[1], ps_o, "po")
-            if ok(c + 2):
-                qk(c + 2, 0)
+            for j in MASKS.get(c, []):
+                maskT_t(j)
             if ok(c + 1):
-                stt(c + 1, 0)
-            if ok(c - LAG):
-                if (c - LAG) % NT == 0:
-                    quant_v((c - LAG) // NT)
-                quant_e(c - LAG)
-                pv(c - LAG)
+                score(c + 1, 0)
+                score(c + 1, 1)
+            if ok(c - 3):
+                quant_e(c - 3)
+            vb, vr = divmod(c + 1, NT)
+            if vb < B and c + 1 >= 0:
+                quant_v(vb, vr)
+            if ok(c - 3):
+                recip(c - 3)
+            if ok(c + 1):
+                rowmin1(c + 1)
             if ok(c):
                 expo(c, 0)
-                e_t(c, 0)
+            if ok(c - 2):
+                evac_e(c - 2)
+            if ok(c):
+                expo(c, 1)
+            if ok(c - 4):
+                o_evac(c - 4)
+                store(c - 4)
+            for u in preps(c - 1):
+                prep_evac(u[0], u[1], "act")
             if ok(c - 1):
-                evac_e(c - 1)
+                e_t(c - 1)
+            for j in MASKS.get(c, []):
+                maskT_evac(j)
             xb, xr = divmod(c + 2, NT)
             if xb < B:
                 regroup_v(xb, xr)
-            if ok(c + 2):
-                qk(c + 2, 1)
-            if ok(c + 1):
-                stt(c + 1, 1)
-                rowmin(c + 1, 0)
-            if ok(c - LAG):
-                recip(c - LAG)
-            if ok(c + 1):
-                rowmin(c + 1, 1)
-            if ok(c):
-                expo(c, 1)
-                e_t(c, 1)
-            if ok(c - LAG):
-                o_evac(c - LAG)
-                store(c - LAG)
-            for u in pl:
-                prep_evac(u[0], u[1], "act")
-            if (c + 2) % NT == 0:
-                nb = (c + 2) // NT + 2
-                if nb < B:
-                    load_kq(nb)
-                    load_v(nb)
+            if c == -2:
+                load_kq(2)
+                load_v(2)
+            nb, cr = divmod(c + 11, NT)
+            if c >= 1 and cr == 0 and nb < B:
+                load_kq(nb)
+                load_v(nb)

@@ -18,7 +18,6 @@ NT = S // P
 NS = B * NT
 FLOPS = 2 * (2 * B * H * S * S * D)
 
-NMM = 12
 U = 2
 
 
@@ -31,9 +30,9 @@ def tile_attention_gear_t_kernel(tc, q, k, v, start_pos, seqlen, mask, out):
         tp = ctx.enter_context(tc.tile_pool(name="tp", bufs=2))
         work = ctx.enter_context(tc.tile_pool(name="work", bufs=3))
         small = ctx.enter_context(tc.tile_pool(name="small", bufs=4))
-        ps_s = ctx.enter_context(tc.psum_pool(name="ps_s", bufs=4))
+        ps_s = ctx.enter_context(tc.psum_pool(name="ps_s", bufs=3))
         ps_t = ctx.enter_context(tc.psum_pool(name="ps_t", bufs=1))
-        ps_e = ctx.enter_context(tc.psum_pool(name="ps_e", bufs=1))
+        ps_e = ctx.enter_context(tc.psum_pool(name="ps_e", bufs=2))
         ps_o = ctx.enter_context(tc.psum_pool(name="ps_o", bufs=2))
 
         st = {}
@@ -70,40 +69,33 @@ def tile_attention_gear_t_kernel(tc, q, k, v, start_pos, seqlen, mask, out):
         warm = const.tile([P, 1], F32, name="warm")
         nc.gpsimd.memset(warm[:], 0.0)
         nc.scalar.activation(out=warm[:], in_=warm[:], func=ACTF.Exp)
-        maskT = const.tile([P, NT, NT, P], F32, name="maskT")
 
         UNITS = [("k", 0), ("q", 0), ("k", 1), ("q", 1)]
 
         def prep_t(b, r, pool, tag):
             which, h = UNITS[r]
-            pt = pool.tile([P, S], F32, tag=tag, name="pt")
-            words = st[(which + "_raw", b)][:].bitcast(F32)
+            pt = pool.tile([P, 2, S], BF16, tag=tag, name="pt")
             for i in range(NT):
-                nc.tensor.transpose(
-                    out=pt[:, i * P:(i + 1) * P],
-                    in_=words[:, i, h * P:(h + 1) * P],
-                    identity=ident_f[:],
-                )
+                for e in range(2):
+                    nc.tensor.transpose(
+                        out=pt[:, e, i * P:(i + 1) * P],
+                        in_=st[(which + "_raw", b)][:, i, h * D + e * P:h * D + (e + 1) * P],
+                        identity=ident_b[:],
+                    )
             st[("pt", b, r)] = pt
 
         def prep_evac(b, r, eng):
             which, h = UNITS[r]
-            dst = tp.tile([P, S], F32, tag="%sT%d" % (which, h), name="dstT")
+            dst = tp.tile([P, 2, S], BF16, tag="%sT%d" % (which, h), name="dstT")
             pt = st[("pt", b, r)]
             if eng == "act":
                 nc.scalar.copy(out=dst[:], in_=pt[:])
             else:
                 nc.vector.tensor_copy(out=dst[:], in_=pt[:])
-            st[(which + "T", b, h)] = dst[:].bitcast(BF16).rearrange("p (s e) -> p s e", e=2)
+            st[(which + "T", b, h)] = dst
 
-        def maskT_t(j):
-            pm = ps_o.tile([P, NT, P], BF16, tag="po", name="pm")
-            for t in range(NT):
-                nc.tensor.transpose(out=pm[:, t, :], in_=mask_sb[:, j, t * P:(t + 1) * P], identity=ident_b[:])
-            st[("pm", j)] = pm
-
-        def maskT_evac(j):
-            nc.scalar.activation(out=maskT[:, j, :, :], in_=st[("pm", j)][:], func=ACTF.Copy, scale=16.0)
+        def pe_mask(n, hh):
+            return hh == 0 and (3 * n) % 8 < 3
 
         def qk(n, hh):
             b, j = divmod(n, NT)
@@ -113,57 +105,45 @@ def tile_attention_gear_t_kernel(tc, q, k, v, start_pos, seqlen, mask, out):
             for e in range(2):
                 nc.tensor.matmul(
                     out=ps[:],
-                    lhsT=qT[:, j * P:(j + 1) * P, e],
-                    rhs=kT[:, :, e],
+                    lhsT=qT[:, e, j * P:(j + 1) * P],
+                    rhs=kT[:, e, :],
                     start=(e == 0),
-                    stop=(e == 1 and hh == 1),
+                    stop=(e == 1 and not pe_mask(n, hh)),
                 )
-            if hh == 0 and n < NMM:
+            if pe_mask(n, hh):
                 nc.tensor.matmul(out=ps[:], lhsT=ident16[:], rhs=mask_sb[:, j, :], start=False, stop=True)
             st[("ps", n, hh)] = ps
-
-        def add_mask(n):
-            if n < NMM:
-                return
-            b, j = divmod(n, NT)
-            ps = st[("ps", n, 0)]
-            for t in range(NT):
-                nc.tensor.matmul(
-                    out=ps[:, t * P:(t + 1) * P],
-                    lhsT=maskT[:, j, t, :],
-                    rhs=ident_f[:],
-                    is_transpose=True,
-                    start=False,
-                    stop=(t == NT - 1),
-                )
 
         def score(n, hh):
             b, j = divmod(n, NT)
             if hh == 0:
                 st[("s2", n)] = work.tile([P, H, S], F32, tag="s2", name="s2")
                 st[("negm", n)] = small.tile([P, H], F32, tag="negm", name="negm")
+            if pe_mask(n, hh):
                 nc.vector.tensor_scalar(
-                    out=st[("s2", n)][:, 0, :],
-                    in0=st[("ps", n, 0)][:],
+                    out=st[("s2", n)][:, hh, :],
+                    in0=st[("ps", n, hh)][:],
                     scalar1=-1.0 / 16.0,
                     scalar2=None,
                     op0=ALU.mult,
                     op1=ALU.min,
-                    accum_out=st[("negm", n)][:, 0:1],
+                    accum_out=st[("negm", n)][:, hh:hh + 1],
                 )
             else:
                 nc.vector.scalar_tensor_tensor(
-                    out=st[("s2", n)][:, 1, :],
-                    in0=st[("ps", n, 1)][:],
+                    out=st[("s2", n)][:, hh, :],
+                    in0=st[("ps", n, hh)][:],
                     scalar=-1.0 / 16.0,
                     in1=mask_sb[:, j, :],
                     op0=ALU.mult,
                     op1=ALU.subtract,
                 )
 
-        def rowmin1(n):
+        def rowmin(n, hh):
+            if pe_mask(n, hh):
+                return
             nc.vector.tensor_reduce(
-                out=st[("negm", n)][:, 1:2], in_=st[("s2", n)][:, 1, :], axis=AX.X, op=ALU.min
+                out=st[("negm", n)][:, hh:hh + 1], in_=st[("s2", n)][:, hh, :], axis=AX.X, op=ALU.min
             )
 
         def expo(n, hh):
@@ -179,17 +159,17 @@ def tile_attention_gear_t_kernel(tc, q, k, v, start_pos, seqlen, mask, out):
                 accum_out=st[("rs", n)][:, hh:hh + 1],
             )
 
-        def e_t(n):
-            pe = ps_e.tile([P, U, H, P], F32, tag="pe", name="pe")
+        def e_t(n, hh):
+            if hh == 0:
+                st[("pe", n)] = ps_e.tile([P, U, H, P], F32, tag="pe", name="pe")
+            pe = st[("pe", n)]
             words = st[("e2", n)][:].bitcast(F32)
-            for hh in range(H):
-                for u in range(U):
-                    nc.tensor.transpose(
-                        out=pe[:, u, hh, :],
-                        in_=words[:, hh, u * P:(u + 1) * P],
-                        identity=ident_f[:],
-                    )
-            st[("pe", n)] = pe
+            for u in range(U):
+                nc.tensor.transpose(
+                    out=pe[:, u, hh, :],
+                    in_=words[:, hh, u * P:(u + 1) * P],
+                    identity=ident_f[:],
+                )
 
         def evac_e(n):
             grp = work.tile([P, H * P, NT], BF16, tag="grp", name="grp", align_bytes=64)
@@ -257,7 +237,7 @@ def tile_attention_gear_t_kernel(tc, q, k, v, start_pos, seqlen, mask, out):
         def o_evac(n):
             ob = work.tile([P, H, D], F32, tag="ob", name="ob", bufs=4)
             st[("ob", n)] = ob
-            if n % 2 == 1:
+            if n % 4 == 1:
                 nc.vector.tensor_tensor(
                     out=ob[:],
                     in0=st[("po", n)][:],
@@ -281,7 +261,7 @@ def tile_attention_gear_t_kernel(tc, q, k, v, start_pos, seqlen, mask, out):
             )
 
         for r in range(4):
-            prep_t(0, r, ps_s, "s")
+            prep_t(0, r, ps_s if r < 3 else ps_t, "s" if r < 3 else "t")
         for r in range(4):
             prep_evac(0, r, "act" if r % 2 == 0 else "dve")
 
@@ -293,8 +273,6 @@ def tile_attention_gear_t_kernel(tc, q, k, v, start_pos, seqlen, mask, out):
                 return [(b1, r)]
             return []
 
-        MASKS = {1: [0], 2: [1], 3: [2, 3]}
-
         for c in range(-2, NS + 5):
             if ok(c + 2):
                 qk(c + 2, 0)
@@ -302,43 +280,40 @@ def tile_attention_gear_t_kernel(tc, q, k, v, start_pos, seqlen, mask, out):
                 pv(c - 4)
             if ok(c + 2):
                 qk(c + 2, 1)
-                add_mask(c + 2)
             for i, u in enumerate(preps(c)):
                 if i == 0:
                     prep_t(u[0], u[1], ps_t, "t")
                 else:
                     prep_t(u[0], u[1], ps_o, "po")
-            for j in MASKS.get(c, []):
-                maskT_t(j)
             if ok(c + 1):
                 score(c + 1, 0)
                 score(c + 1, 1)
             if ok(c - 3):
                 quant_e(c - 3)
             vb, vr = divmod(c + 1, NT)
-            if vb < B and c + 1 >= 0:
+            if 0 <= vb < B:
                 quant_v(vb, vr)
             if ok(c - 3):
                 recip(c - 3)
             if ok(c + 1):
-                rowmin1(c + 1)
+                rowmin(c + 1, 0)
+                rowmin(c + 1, 1)
             if ok(c):
                 expo(c, 0)
-            if ok(c - 2):
-                evac_e(c - 2)
+            for u in preps(c - 1):
+                prep_evac(u[0], u[1], "act")
             if ok(c):
                 expo(c, 1)
+            if ok(c - 2):
+                evac_e(c - 2)
             if ok(c - 4):
                 o_evac(c - 4)
                 store(c - 4)
-            for u in preps(c - 1):
-                prep_evac(u[0], u[1], "act")
             if ok(c - 1):
-                e_t(c - 1)
-            for j in MASKS.get(c, []):
-                maskT_evac(j)
+                e_t(c - 1, 0)
+                e_t(c - 1, 1)
             xb, xr = divmod(c + 2, NT)
-            if xb < B:
+            if 0 <= xb < B:
                 regroup_v(xb, xr)
             if c == -2:
                 load_kq(2)

@@ -53,12 +53,24 @@ def tile_attention_gear_t_kernel(tc, q, k, v, start_pos, seqlen, mask, out):
             nc.sync.dma_start(out=v_raw[:], in_=v[b].rearrange("(p t) h d -> p t (h d)", t=NT))
             st[("v_raw", b)] = v_raw
 
-        load_kq(0)
+        k_raw0 = raw.tile([P, NT, H * D], BF16, tag="k_raw", name="k_raw0")
+        q_raw0 = raw.tile([P, NT, H * D], BF16, tag="q_raw", name="q_raw0")
+        st[("k_raw", 0)] = k_raw0
+        st[("q_raw", 0)] = q_raw0
         mask_sb = const.tile([P, NT, S], BF16, name="mask_sb")
-        nc.sync.dma_start(out=mask_sb[:], in_=mask[0, 0].rearrange("(p j) c -> p j c", j=NT))
+        mask_pj = mask[0, 0].rearrange("(p j) c -> p j c", j=NT)
+        for hh in range(H):
+            ds = slice(hh * D, (hh + 1) * D)
+            nc.sync.dma_start(out=k_raw0[:, :, ds], in_=k[0].rearrange("(t p) h d -> p t (h d)", p=P)[:, :, ds])
+            nc.sync.dma_start(out=q_raw0[:, :, ds], in_=q[0].rearrange("(p j) h d -> p j (h d)", j=NT)[:, :, ds])
+            if hh == 0:
+                nc.sync.dma_start(out=mask_sb[:, 0, :], in_=mask_pj[:, 0, :])
+        nc.sync.dma_start(out=mask_sb[:, 1:, :], in_=mask_pj[:, 1:, :])
         load_kq(1)
         load_v(0)
         load_v(1)
+        load_kq(2)
+        load_v(2)
 
         ident_f = const.tile([P, P], F32, name="ident_f")
         make_identity(nc, ident_f[:])
@@ -260,10 +272,17 @@ def tile_attention_gear_t_kernel(tc, q, k, v, start_pos, seqlen, mask, out):
                 in_=st[("ob", n)][:].rearrange("p h d -> p (h d)"),
             )
 
-        for r in range(4):
-            prep_t(0, r, ps_s if r < 3 else ps_t, "s" if r < 3 else "t")
-        for r in range(4):
-            prep_evac(0, r, "act" if r % 2 == 0 else "dve")
+        prep_t(0, 0, ps_s, "s")
+        prep_t(0, 1, ps_s, "s")
+        prep_t(0, 2, ps_s, "s")
+        prep_evac(0, 0, "act")
+        prep_evac(0, 1, "dve")
+        prep_evac(0, 2, "act")
+        prep_t(0, 3, ps_t, "t")
+        prep_evac(0, 3, "act")
+        qk(0, 0)
+        qk(0, 1)
+        regroup_v(0, 0)
 
         def preps(c):
             if c in (-1, 0):
@@ -273,11 +292,34 @@ def tile_attention_gear_t_kernel(tc, q, k, v, start_pos, seqlen, mask, out):
                 return [(b1, r)]
             return []
 
-        for c in range(-2, NS + 5):
+        def due(c, lag):
+            s = SHORT + lag - 1
+            if c < s:
+                ns = [c - lag]
+            elif c == s:
+                ns = [c - lag, c - lag + 1]
+            else:
+                ns = [c - lag + 1]
+            return [n for n in ns if ok(n)]
+
+        SHORT = 27
+        for c in range(-1, NS + 5):
+            if ok(c + 1):
+                score(c + 1, 0)
+                score(c + 1, 1)
+            for n in due(c, 3):
+                quant_e(n)
+                recip(n)
+            if ok(c + 1):
+                rowmin(c + 1, 0)
+                rowmin(c + 1, 1)
+            vb, vr = divmod(c, NT)
+            if 0 <= vb < B:
+                quant_v(vb, vr)
             if ok(c + 2):
                 qk(c + 2, 0)
-            if ok(c - 4):
-                pv(c - 4)
+            for n in due(c, 4):
+                pv(n)
             if ok(c + 2):
                 qk(c + 2, 1)
             for i, u in enumerate(preps(c)):
@@ -285,39 +327,22 @@ def tile_attention_gear_t_kernel(tc, q, k, v, start_pos, seqlen, mask, out):
                     prep_t(u[0], u[1], ps_t, "t")
                 else:
                     prep_t(u[0], u[1], ps_o, "po")
-            if ok(c + 1):
-                score(c + 1, 0)
-                score(c + 1, 1)
-            if ok(c - 3):
-                quant_e(c - 3)
-            vb, vr = divmod(c + 1, NT)
-            if 0 <= vb < B:
-                quant_v(vb, vr)
-            if ok(c - 3):
-                recip(c - 3)
-            if ok(c + 1):
-                rowmin(c + 1, 0)
-                rowmin(c + 1, 1)
             if ok(c):
                 expo(c, 0)
+                expo(c, 1)
             for u in preps(c - 1):
                 prep_evac(u[0], u[1], "act")
-            if ok(c):
-                expo(c, 1)
-            if ok(c - 2):
-                evac_e(c - 2)
-            if ok(c - 4):
-                o_evac(c - 4)
-                store(c - 4)
-            if ok(c - 1):
-                e_t(c - 1, 0)
-                e_t(c - 1, 1)
+            for n in due(c, 2):
+                evac_e(n)
+            for n in due(c, 4):
+                o_evac(n)
+                store(n)
+            for n in due(c, 1):
+                e_t(n, 0)
+                e_t(n, 1)
             xb, xr = divmod(c + 2, NT)
             if 0 <= xb < B:
                 regroup_v(xb, xr)
-            if c == -2:
-                load_kq(2)
-                load_v(2)
             nb, cr = divmod(c + 11, NT)
             if c >= 1 and cr == 0 and nb < B:
                 load_kq(nb)

@@ -86,25 +86,25 @@ def tile_attention_gear_t_kernel(tc, q, k, v, start_pos, seqlen, mask, out):
 
         def prep_t(b, r, pool, tag):
             which, h = UNITS[r]
-            pt = pool.tile([P, 2, S], BF16, tag=tag, name="pt")
+            pt = pool.tile([P, S], F32, tag=tag, name="pt")
+            words = st[(which + "_raw", b)][:].bitcast(F32)
             for i in range(NT):
-                for e in range(2):
-                    nc.tensor.transpose(
-                        out=pt[:, e, i * P:(i + 1) * P],
-                        in_=st[(which + "_raw", b)][:, i, h * D + e * P:h * D + (e + 1) * P],
-                        identity=ident_b[:],
-                    )
+                nc.tensor.transpose(
+                    out=pt[:, i * P:(i + 1) * P],
+                    in_=words[:, i, h * P:(h + 1) * P],
+                    identity=ident_f[:],
+                )
             st[("pt", b, r)] = pt
 
         def prep_evac(b, r, eng):
             which, h = UNITS[r]
-            dst = tp.tile([P, 2, S], BF16, tag="%sT%d" % (which, h), name="dstT")
+            dst = tp.tile([P, S], F32, tag="%sT%d" % (which, h), name="dstT")
             pt = st[("pt", b, r)]
             if eng == "act":
                 nc.scalar.copy(out=dst[:], in_=pt[:])
             else:
                 nc.vector.tensor_copy(out=dst[:], in_=pt[:])
-            st[(which + "T", b, h)] = dst
+            st[(which + "T", b, h)] = dst[:].bitcast(BF16).rearrange("p (s e) -> p s e", e=2)
 
         def pe_mask(n, hh):
             return hh == 0 and (3 * n) % 8 < 3
@@ -117,8 +117,8 @@ def tile_attention_gear_t_kernel(tc, q, k, v, start_pos, seqlen, mask, out):
             for e in range(2):
                 nc.tensor.matmul(
                     out=ps[:],
-                    lhsT=qT[:, e, j * P:(j + 1) * P],
-                    rhs=kT[:, e, :],
+                    lhsT=qT[:, j * P:(j + 1) * P, e],
+                    rhs=kT[:, :, e],
                     start=(e == 0),
                     stop=(e == 1 and not pe_mask(n, hh)),
                 )

@@ -208,11 +208,11 @@ def tile_attention_gear_t_kernel(tc, q, k, v, start_pos, seqlen, mask, out):
             st[("rc", n)] = rc
 
         def regroup_v(b, r):
-            if r == 0:
-                st[("vgrp", b)] = work.tile([P, H * D, NT], BF16, tag="vgrp", name="vgrp", bufs=2, align_bytes=64)
+            vg = work.tile([P, P, NT], BF16, tag="vgrp", name="vgrp", bufs=2, align_bytes=64)
+            st[("vgrp", b, r)] = vg
             cs = slice(r * P, (r + 1) * P)
             nc.gpsimd.tensor_scalar(
-                out=st[("vgrp", b)][:, cs, :],
+                out=vg[:],
                 in0=st[("v_raw", b)][:, :, cs].rearrange("p t c -> p c t"),
                 scalar1=1.0,
                 scalar2=0.0,
@@ -228,7 +228,7 @@ def tile_attention_gear_t_kernel(tc, q, k, v, start_pos, seqlen, mask, out):
             nc.vector.quantize_mx(
                 out=st[("vc", b)][:, cs].bitcast(FP8X4),
                 scales=st[("vs", b)][:, cs],
-                in_=st[("vgrp", b)][:, cs, :].rearrange("p c t -> p (c t)"),
+                in_=st[("vgrp", b, r)][:].rearrange("p c t -> p (c t)"),
             )
 
         def pv(n):
@@ -309,13 +309,14 @@ def tile_attention_gear_t_kernel(tc, q, k, v, start_pos, seqlen, mask, out):
                 score(c + 1, 1)
             for n in due(c, 3):
                 quant_e(n)
+            vb, vr = divmod(c, NT)
+            if 0 <= vb < B:
+                quant_v(vb, vr)
+            for n in due(c, 3):
                 recip(n)
             if ok(c + 1):
                 rowmin(c + 1, 0)
                 rowmin(c + 1, 1)
-            vb, vr = divmod(c, NT)
-            if 0 <= vb < B:
-                quant_v(vb, vr)
             if ok(c + 2):
                 qk(c + 2, 0)
             for n in due(c, 4):

@@ -18,6 +18,7 @@ NT = S // P
 NS = B * NT
 FLOPS = 2 * (2 * B * H * S * S * D)
 
+NMM = 12
 U = 2
 
 
@@ -59,12 +60,16 @@ def tile_attention_gear_t_kernel(tc, q, k, v, start_pos, seqlen, mask, out):
         st[("q_raw", 0)] = q_raw0
         mask_sb = const.tile([P, NT, S], BF16, name="mask_sb")
         mask_pj = mask[0, 0].rearrange("(p j) c -> p j c", j=NT)
+        k_tp = k[0].rearrange("(t p) h d -> p t (h d)", p=P)
+        q_pj = q[0].rearrange("(p j) h d -> p j (h d)", j=NT)
         for hh in range(H):
             ds = slice(hh * D, (hh + 1) * D)
-            nc.sync.dma_start(out=k_raw0[:, :, ds], in_=k[0].rearrange("(t p) h d -> p t (h d)", p=P)[:, :, ds])
-            nc.sync.dma_start(out=q_raw0[:, :, ds], in_=q[0].rearrange("(p j) h d -> p j (h d)", j=NT)[:, :, ds])
+            nc.sync.dma_start(out=q_raw0[:, 0, ds], in_=q_pj[:, 0, ds])
+            for t in range(0, NT, 2):
+                nc.sync.dma_start(out=k_raw0[:, t:t + 2, ds], in_=k_tp[:, t:t + 2, ds])
             if hh == 0:
                 nc.sync.dma_start(out=mask_sb[:, 0, :], in_=mask_pj[:, 0, :])
+        nc.sync.dma_start(out=q_raw0[:, 1:, :], in_=q_pj[:, 1:, :])
         nc.sync.dma_start(out=mask_sb[:, 1:, :], in_=mask_pj[:, 1:, :])
         load_kq(1)
         load_v(0)
@@ -72,17 +77,48 @@ def tile_attention_gear_t_kernel(tc, q, k, v, start_pos, seqlen, mask, out):
         load_kq(2)
         load_v(2)
 
-        ident_f = const.tile([P, P], F32, name="ident_f")
-        make_identity(nc, ident_f[:])
         ident_b = const.tile([P, P], BF16, name="ident_b")
         make_identity(nc, ident_b[:])
+        ident_f = const.tile([P, P], F32, name="ident_f")
+        make_identity(nc, ident_f[:])
         ident16 = const.tile([P, P], BF16, name="ident16")
         nc.gpsimd.tensor_scalar(out=ident16[:], in0=ident_b[:], scalar1=16.0, scalar2=0.0, op0=ALU.mult, op1=ALU.add)
+        maskT = const.tile([P, NT, NT, P], F32, name="maskT")
         warm = const.tile([P, 1], F32, name="warm")
         nc.gpsimd.memset(warm[:], 0.0)
         nc.scalar.activation(out=warm[:], in_=warm[:], func=ACTF.Exp)
 
         UNITS = [("k", 0), ("q", 0), ("k", 1), ("q", 1)]
+
+        qT0 = [tp.tile([P, 2, S], BF16, tag="qT%d" % hh, name="qT0") for hh in range(H)]
+        kT0 = [tp.tile([P, 2, S], BF16, tag="kT%d" % hh, name="kT0") for hh in range(H)]
+        for hh in range(H):
+            st[("qT", 0, hh)] = qT0[hh][:].rearrange("p e s -> p s e")
+            st[("kT", 0, hh)] = kT0[hh][:].rearrange("p e s -> p s e")
+
+        def copy_out(on_vector, dst, src):
+            if on_vector:
+                nc.vector.tensor_copy(out=dst, in_=src)
+            else:
+                nc.scalar.copy(out=dst, in_=src)
+
+        def k0_part(hh, e, pool, tag, on_vector):
+            pt = pool.tile([P, S], BF16, tag=tag, name="ptk")
+            for i in range(NT):
+                cs = slice(hh * D + e * P, hh * D + (e + 1) * P)
+                nc.tensor.transpose(out=pt[:, i * P:(i + 1) * P], in_=k_raw0[:, i, cs], identity=ident_b[:])
+            copy_out(on_vector, kT0[hh][:, e, :], pt[:])
+
+        def q0_part(hh, j0, j1, pool, tag, on_vector):
+            pt = pool.tile([P, 2, (j1 - j0) * P], BF16, tag=tag, name="ptq")
+            for j in range(j0, j1):
+                for e in range(2):
+                    nc.tensor.transpose(
+                        out=pt[:, e, (j - j0) * P:(j - j0 + 1) * P],
+                        in_=q_raw0[:, j, hh * D + e * P:hh * D + (e + 1) * P],
+                        identity=ident_b[:],
+                    )
+            copy_out(on_vector, qT0[hh][:, :, j0 * P:j1 * P], pt[:])
 
         def prep_t(b, r, pool, tag):
             which, h = UNITS[r]
@@ -98,7 +134,8 @@ def tile_attention_gear_t_kernel(tc, q, k, v, start_pos, seqlen, mask, out):
 
         def prep_evac(b, r, eng):
             which, h = UNITS[r]
-            dst = tp.tile([P, S], F32, tag="%sT%d" % (which, h), name="dstT")
+            tag = "%sT%d" % (which, h)
+            dst = tp.tile([P, S], F32, tag=tag, name="dstT")
             pt = st[("pt", b, r)]
             if eng == "act":
                 nc.scalar.copy(out=dst[:], in_=pt[:])
@@ -106,8 +143,19 @@ def tile_attention_gear_t_kernel(tc, q, k, v, start_pos, seqlen, mask, out):
                 nc.vector.tensor_copy(out=dst[:], in_=pt[:])
             st[(which + "T", b, h)] = dst[:].bitcast(BF16).rearrange("p (s e) -> p s e", e=2)
 
+        def maskT_t(j):
+            pm = ps_o.tile([P, NT, P], BF16, tag="po", name="pm")
+            for t in range(NT):
+                nc.tensor.transpose(out=pm[:, t, :], in_=mask_sb[:, j, t * P:(t + 1) * P], identity=ident_b[:])
+            st[("pm", j)] = pm
+
+        def maskT_evac(j):
+            nc.vector.tensor_scalar(
+                out=maskT[:, j, :, :], in0=st[("pm", j)][:], scalar1=16.0, scalar2=0.0, op0=ALU.mult, op1=ALU.add
+            )
+
         def pe_mask(n, hh):
-            return hh == 0 and (3 * n) % 8 < 3
+            return hh == 0
 
         def qk(n, hh):
             b, j = divmod(n, NT)
@@ -122,9 +170,23 @@ def tile_attention_gear_t_kernel(tc, q, k, v, start_pos, seqlen, mask, out):
                     start=(e == 0),
                     stop=(e == 1 and not pe_mask(n, hh)),
                 )
-            if pe_mask(n, hh):
+            if hh == 0 and n < NMM:
                 nc.tensor.matmul(out=ps[:], lhsT=ident16[:], rhs=mask_sb[:, j, :], start=False, stop=True)
             st[("ps", n, hh)] = ps
+
+        def add_mask(n):
+            b, j = divmod(n, NT)
+            if n < NMM:
+                return
+            for t in range(NT):
+                nc.tensor.matmul(
+                    out=st[("ps", n, 0)][:, t * P:(t + 1) * P],
+                    lhsT=maskT[:, j, t, :],
+                    rhs=ident_f[:],
+                    is_transpose=True,
+                    start=False,
+                    stop=(t == NT - 1),
+                )
 
         def score(n, hh):
             b, j = divmod(n, NT)
@@ -152,8 +214,6 @@ def tile_attention_gear_t_kernel(tc, q, k, v, start_pos, seqlen, mask, out):
                 )
 
         def rowmin(n, hh):
-            if pe_mask(n, hh):
-                return
             nc.vector.tensor_reduce(
                 out=st[("negm", n)][:, hh:hh + 1], in_=st[("s2", n)][:, hh, :], axis=AX.X, op=ALU.min
             )
@@ -183,12 +243,13 @@ def tile_attention_gear_t_kernel(tc, q, k, v, start_pos, seqlen, mask, out):
                     identity=ident_f[:],
                 )
 
-        def evac_e(n):
+        def evac_e(n, on_vector):
             grp = work.tile([P, H * P, NT], BF16, tag="grp", name="grp", align_bytes=64)
-            nc.scalar.copy(
-                out=grp[:].bitcast(F32),
-                in_=st[("pe", n)][:].rearrange("p u h c -> p (h c) u"),
-            )
+            src = st[("pe", n)][:].rearrange("p u h c -> p (h c) u")
+            if on_vector:
+                nc.vector.tensor_copy(out=grp[:].bitcast(F32), in_=src)
+            else:
+                nc.scalar.copy(out=grp[:].bitcast(F32), in_=src)
             st[("grp", n)] = grp
 
         def quant_e(n):
@@ -246,10 +307,10 @@ def tile_attention_gear_t_kernel(tc, q, k, v, start_pos, seqlen, mask, out):
                 )
             st[("po", n)] = po
 
-        def o_evac(n):
+        def o_evac(n, on_vector):
             ob = work.tile([P, H, D], F32, tag="ob", name="ob", bufs=4)
             st[("ob", n)] = ob
-            if n % 4 == 1:
+            if on_vector:
                 nc.vector.tensor_tensor(
                     out=ob[:],
                     in0=st[("po", n)][:],
@@ -272,16 +333,16 @@ def tile_attention_gear_t_kernel(tc, q, k, v, start_pos, seqlen, mask, out):
                 in_=st[("ob", n)][:].rearrange("p h d -> p (h d)"),
             )
 
-        prep_t(0, 0, ps_s, "s")
-        prep_t(0, 1, ps_s, "s")
-        prep_t(0, 2, ps_s, "s")
-        prep_evac(0, 0, "act")
-        prep_evac(0, 1, "dve")
-        prep_evac(0, 2, "act")
-        prep_t(0, 3, ps_t, "t")
-        prep_evac(0, 3, "act")
+        q0_part(0, 0, 1, ps_t, "t", True)
+        k0_part(0, 0, ps_s, "s", False)
+        k0_part(0, 1, ps_s, "s", True)
+        q0_part(1, 0, 1, ps_o, "po", True)
+        k0_part(1, 0, ps_e, "pe", False)
+        k0_part(1, 1, ps_e, "pe", True)
         qk(0, 0)
+        q0_part(0, 1, NT, ps_t, "t", False)
         qk(0, 1)
+        q0_part(1, 1, NT, ps_o, "po", False)
         regroup_v(0, 0)
 
         def preps(c):
@@ -292,37 +353,30 @@ def tile_attention_gear_t_kernel(tc, q, k, v, start_pos, seqlen, mask, out):
                 return [(b1, r)]
             return []
 
-        def due(c, lag):
-            s = SHORT + lag - 1
-            if c < s:
-                ns = [c - lag]
-            elif c == s:
-                ns = [c - lag, c - lag + 1]
-            else:
-                ns = [c - lag + 1]
-            return [n for n in ns if ok(n)]
-
-        SHORT = 27
-        for c in range(-1, NS + 5):
+        MASKS = {1: [0], 2: [1], 3: [2, 3]}
+        for c in range(-1, NS - 1):
             if ok(c + 1):
                 score(c + 1, 0)
                 score(c + 1, 1)
-            for n in due(c, 3):
-                quant_e(n)
+            if c + 1 == NS - 1:
+                rowmin(c + 1, 1)
+            if ok(c - 3):
+                recip(c - 3)
+                quant_e(c - 3)
             vb, vr = divmod(c, NT)
             if 0 <= vb < B:
                 quant_v(vb, vr)
-            for n in due(c, 3):
-                recip(n)
-            if ok(c + 1):
-                rowmin(c + 1, 0)
+            if c + 1 < NS - 1:
                 rowmin(c + 1, 1)
             if ok(c + 2):
                 qk(c + 2, 0)
-            for n in due(c, 4):
-                pv(n)
+            if ok(c - 4):
+                pv(c - 4)
             if ok(c + 2):
                 qk(c + 2, 1)
+                add_mask(c + 2)
+            for j in MASKS.get(c, []):
+                maskT_t(j)
             for i, u in enumerate(preps(c)):
                 if i == 0:
                     prep_t(u[0], u[1], ps_t, "t")
@@ -333,14 +387,16 @@ def tile_attention_gear_t_kernel(tc, q, k, v, start_pos, seqlen, mask, out):
                 expo(c, 1)
             for u in preps(c - 1):
                 prep_evac(u[0], u[1], "act")
-            for n in due(c, 2):
-                evac_e(n)
-            for n in due(c, 4):
-                o_evac(n)
-                store(n)
-            for n in due(c, 1):
-                e_t(n, 0)
-                e_t(n, 1)
+            if ok(c - 2):
+                evac_e(c - 2, False)
+            if ok(c - 4):
+                o_evac(c - 4, c % 2 == 1)
+                store(c - 4)
+            if ok(c - 1):
+                e_t(c - 1, 0)
+                e_t(c - 1, 1)
+            for j in MASKS.get(c, []):
+                maskT_evac(j)
             xb, xr = divmod(c + 2, NT)
             if 0 <= xb < B:
                 regroup_v(xb, xr)
@@ -348,3 +404,93 @@ def tile_attention_gear_t_kernel(tc, q, k, v, start_pos, seqlen, mask, out):
             if c >= 1 and cr == 0 and nb < B:
                 load_kq(nb)
                 load_v(nb)
+
+        z = NS - 1
+        zb = B - 1
+
+        def z_e_t(hh):
+            pe = ps_s.tile([P, U, P], F32, tag="s", name="zpe")
+            words = st[("e2", z)][:].bitcast(F32)
+            for u in range(U):
+                nc.tensor.transpose(out=pe[:, u, :], in_=words[:, hh, u * P:(u + 1) * P], identity=ident_f[:])
+            st[("zpe", hh)] = pe
+
+        def z_evac(hh, on_vector):
+            grp = work.tile([P, P, NT], BF16, tag="zgrp", name="zgrp", bufs=2, align_bytes=64)
+            src = st[("zpe", hh)][:].rearrange("p u c -> p c u")
+            if on_vector:
+                nc.vector.tensor_copy(out=grp[:].bitcast(F32), in_=src)
+            else:
+                nc.scalar.copy(out=grp[:].bitcast(F32), in_=src)
+            st[("zgrp", hh)] = grp
+
+        def z_quant(hh):
+            ec = work.tile([P, P], U32, tag="zec", name="zec", bufs=2, align_bytes=64)
+            es = work.tile([P, P], U8, tag="zes", name="zes", bufs=2, align_bytes=64)
+            nc.vector.quantize_mx(
+                out=ec[:].bitcast(FP8X4),
+                scales=es[:],
+                in_=st[("zgrp", hh)][:].rearrange("p c t -> p (c t)"),
+            )
+            st[("zec", hh)] = ec
+            st[("zes", hh)] = es
+
+        def z_pv(hh):
+            po = ps_s.tile([P, D], F32, tag="s", name="zpo")
+            nc.tensor.matmul_mx(
+                out=po[:],
+                lhsT=st[("zec", hh)][:].bitcast(FP8X4),
+                lhsT_scale=st[("zes", hh)][:],
+                rhs=st[("vc", zb)][:, hh * D:(hh + 1) * D].bitcast(FP8X4),
+                rhs_scale=st[("vs", zb)][:, hh * D:(hh + 1) * D],
+                start=True,
+                stop=True,
+            )
+            st[("zpo", hh)] = po
+
+        def z_out(hh, on_vector):
+            ob = work.tile([P, D], F32, tag="zob", name="zob", bufs=2)
+            po = st[("zpo", hh)]
+            sc = st[("rc", z)][:, hh:hh + 1]
+            if on_vector:
+                nc.vector.tensor_scalar(out=ob[:], in0=po[:], scalar1=sc, scalar2=None, op0=ALU.mult)
+            else:
+                nc.scalar.activation(out=ob[:], in_=po[:], func=ACTF.Copy, scale=sc)
+            nc.sync.dma_start(out=out[zb].rearrange("(p j) h d -> p j h d", j=NT)[:, NT - 1, hh, :], in_=ob[:])
+
+        e_t(z - 1, 0)
+        e_t(z - 1, 1)
+        quant_v(zb, NT - 1)
+        recip(z - 3)
+        quant_e(z - 3)
+        pv(z - 4)
+        expo(z, 0)
+        evac_e(z - 2, False)
+        expo(z, 1)
+        z_e_t(0)
+        o_evac(z - 4, True)
+        store(z - 4)
+        pv(z - 3)
+        z_evac(0, True)
+        z_e_t(1)
+        evac_e(z - 1, False)
+        z_evac(1, False)
+        recip(z - 2)
+        quant_e(z - 2)
+        z_quant(0)
+        recip(z)
+        z_quant(1)
+        pv(z - 2)
+        z_pv(0)
+        z_pv(1)
+        o_evac(z - 3, False)
+        store(z - 3)
+        recip(z - 1)
+        quant_e(z - 1)
+        pv(z - 1)
+        o_evac(z - 2, True)
+        store(z - 2)
+        z_out(1, False)
+        z_out(0, True)
+        o_evac(z - 1, False)
+        store(z - 1)

@@ -150,37 +150,39 @@ def tile_attention_gear_t_kernel(tc, q, k, v, start_pos, seqlen, mask, out):
             st[("pm", j)] = pm
 
         def maskT_evac(j):
-            nc.vector.tensor_scalar(
-                out=maskT[:, j, :, :], in0=st[("pm", j)][:], scalar1=16.0, scalar2=0.0, op0=ALU.mult, op1=ALU.add
+            mb = work.tile([P, NT, P], BF16, tag="mb", name="mb", bufs=2)
+            nc.vector.tensor_copy(out=mb[:], in_=st[("pm", j)][:])
+            nc.gpsimd.tensor_scalar(
+                out=maskT[:, j, :, :], in0=mb[:], scalar1=16.0, scalar2=0.0, op0=ALU.mult, op1=ALU.add
             )
 
         def pe_mask(n, hh):
-            return hh == 0
+            return hh == 0 or (n >= 8 and n % 8 == 4)
+
+        def qk_pass(n, hh, e):
+            b, j = divmod(n, NT)
+            if e == 0:
+                st[("ps", n, hh)] = ps_s.tile([P, S], F32, tag="s", name="ps")
+            ps = st[("ps", n, hh)]
+            nc.tensor.matmul(
+                out=ps[:],
+                lhsT=st[("qT", b, hh)][:, j * P:(j + 1) * P, e],
+                rhs=st[("kT", b, hh)][:, :, e],
+                start=(e == 0),
+                stop=(e == 1 and not pe_mask(n, hh)),
+            )
+            if e == 1 and hh == 0 and n < NMM:
+                nc.tensor.matmul(out=ps[:], lhsT=ident16[:], rhs=mask_sb[:, j, :], start=False, stop=True)
 
         def qk(n, hh):
-            b, j = divmod(n, NT)
-            ps = ps_s.tile([P, S], F32, tag="s", name="ps")
-            qT = st[("qT", b, hh)]
-            kT = st[("kT", b, hh)]
-            for e in range(2):
-                nc.tensor.matmul(
-                    out=ps[:],
-                    lhsT=qT[:, j * P:(j + 1) * P, e],
-                    rhs=kT[:, :, e],
-                    start=(e == 0),
-                    stop=(e == 1 and not pe_mask(n, hh)),
-                )
-            if hh == 0 and n < NMM:
-                nc.tensor.matmul(out=ps[:], lhsT=ident16[:], rhs=mask_sb[:, j, :], start=False, stop=True)
-            st[("ps", n, hh)] = ps
+            qk_pass(n, hh, 0)
+            qk_pass(n, hh, 1)
 
-        def add_mask(n):
+        def add_mask(n, hh):
             b, j = divmod(n, NT)
-            if n < NMM:
-                return
             for t in range(NT):
                 nc.tensor.matmul(
-                    out=st[("ps", n, 0)][:, t * P:(t + 1) * P],
+                    out=st[("ps", n, hh)][:, t * P:(t + 1) * P],
                     lhsT=maskT[:, j, t, :],
                     rhs=ident_f[:],
                     is_transpose=True,
@@ -221,27 +223,25 @@ def tile_attention_gear_t_kernel(tc, q, k, v, start_pos, seqlen, mask, out):
         def expo(n, hh):
             if hh == 0:
                 st[("e2", n)] = work.tile([P, H, S], BF16, tag="e2", name="e2")
-                st[("rs", n)] = small.tile([P, H], F32, tag="rs", name="rs", bufs=6)
+                if n % 2 == 0:
+                    st[("rs", n // 2)] = small.tile([P, 2, H], F32, tag="rs", name="rs", bufs=4)
             nc.scalar.activation(
                 out=st[("e2", n)][:, hh, :].rearrange("p (u w e) -> p u w e", u=U, e=2),
                 in_=st[("s2", n)][:, hh, :].rearrange("p (w u e) -> p u w e", u=U, e=2),
                 func=ACTF.Exp,
                 bias=st[("negm", n)][:, hh:hh + 1],
                 scale=-1.0,
-                accum_out=st[("rs", n)][:, hh:hh + 1],
+                accum_out=st[("rs", n // 2)][:, n % 2, hh:hh + 1],
             )
 
-        def e_t(n, hh):
-            if hh == 0:
+        def e_t(n, hh, u):
+            if hh == 0 and u == 0:
                 st[("pe", n)] = ps_e.tile([P, U, H, P], F32, tag="pe", name="pe")
-            pe = st[("pe", n)]
-            words = st[("e2", n)][:].bitcast(F32)
-            for u in range(U):
-                nc.tensor.transpose(
-                    out=pe[:, u, hh, :],
-                    in_=words[:, hh, u * P:(u + 1) * P],
-                    identity=ident_f[:],
-                )
+            nc.tensor.transpose(
+                out=st[("pe", n)][:, u, hh, :],
+                in_=st[("e2", n)][:].bitcast(F32)[:, hh, u * P:(u + 1) * P],
+                identity=ident_f[:],
+            )
 
         def evac_e(n, on_vector):
             grp = work.tile([P, H * P, NT], BF16, tag="grp", name="grp", align_bytes=64)
@@ -263,10 +263,11 @@ def tile_attention_gear_t_kernel(tc, q, k, v, start_pos, seqlen, mask, out):
             st[("ec", n)] = ec
             st[("es", n)] = es
 
-        def recip(n):
-            rc = small.tile([P, H], F32, tag="rc", name="rc")
-            nc.vector.reciprocal(out=rc[:], in_=st[("rs", n)][:])
-            st[("rc", n)] = rc
+        def recip(m):
+            rc = small.tile([P, 2, H], F32, tag="rc", name="rc")
+            nc.vector.reciprocal(out=rc[:], in_=st[("rs", m)][:])
+            st[("rc", 2 * m)] = rc[:, 0, :]
+            st[("rc", 2 * m + 1)] = rc[:, 1, :]
 
         def regroup_v(b, r):
             vg = work.tile([P, P, NT], BF16, tag="vgrp", name="vgrp", bufs=2, align_bytes=64)
@@ -307,24 +308,16 @@ def tile_attention_gear_t_kernel(tc, q, k, v, start_pos, seqlen, mask, out):
                 )
             st[("po", n)] = po
 
-        def o_evac(n, on_vector):
-            ob = work.tile([P, H, D], F32, tag="ob", name="ob", bufs=4)
-            st[("ob", n)] = ob
+        def scaled_copy(on_vector, dst, src, sc):
             if on_vector:
-                nc.vector.tensor_tensor(
-                    out=ob[:],
-                    in0=st[("po", n)][:],
-                    in1=st[("rc", n)][:].unsqueeze(2).to_broadcast([P, H, D]),
-                    op=ALU.mult,
-                )
-                return
-            for hh in range(H):
-                nc.scalar.activation(
-                    out=ob[:, hh, :],
-                    in_=st[("po", n)][:, hh, :],
-                    func=ACTF.Copy,
-                    scale=st[("rc", n)][:, hh:hh + 1],
-                )
+                nc.vector.tensor_scalar(out=dst, in0=src, scalar1=sc, scalar2=None, op0=ALU.mult)
+            else:
+                nc.scalar.activation(out=dst, in_=src, func=ACTF.Copy, scale=sc)
+
+        def o_evac(n, hh, on_vector):
+            if ("ob", n) not in st:
+                st[("ob", n)] = work.tile([P, H, D], F32, tag="ob", name="ob", bufs=4)
+            scaled_copy(on_vector, st[("ob", n)][:, hh, :], st[("po", n)][:, hh, :], st[("rc", n)][:, hh:hh + 1])
 
         def store(n):
             b, j = divmod(n, NT)
@@ -353,28 +346,43 @@ def tile_attention_gear_t_kernel(tc, q, k, v, start_pos, seqlen, mask, out):
                 return [(b1, r)]
             return []
 
-        MASKS = {1: [0], 2: [1], 3: [2, 3]}
+        def both_on_vector(n):
+            return n >= 6 and n % 8 == 6
+
+        MASKS = {1: [0], 2: [1, 2], 3: [3]}
         for c in range(-1, NS - 1):
             if ok(c + 1):
                 score(c + 1, 0)
                 score(c + 1, 1)
+            if ok(c - 5):
+                if both_on_vector(c - 5):
+                    o_evac(c - 5, 0, True)
+                o_evac(c - 5, 1, True)
+                store(c - 5)
             if c + 1 == NS - 1:
                 rowmin(c + 1, 1)
             if ok(c - 3):
-                recip(c - 3)
+                if c % 2 == 1:
+                    recip((c - 3) // 2)
                 quant_e(c - 3)
             vb, vr = divmod(c, NT)
-            if 0 <= vb < B:
+            if c > 0:
                 quant_v(vb, vr)
-            if c + 1 < NS - 1:
+            if c + 1 < NS - 1 and not pe_mask(c + 1, 1):
                 rowmin(c + 1, 1)
-            if ok(c + 2):
+            if c == 0:
+                quant_v(0, 0)
+            scores = ok(c + 2)
+            if scores:
                 qk(c + 2, 0)
             if ok(c - 4):
                 pv(c - 4)
-            if ok(c + 2):
+            if scores:
                 qk(c + 2, 1)
-                add_mask(c + 2)
+            if scores:
+                for hh in range(H):
+                    if pe_mask(c + 2, hh) and (hh == 1 or c + 2 >= NMM):
+                        add_mask(c + 2, hh)
             for j in MASKS.get(c, []):
                 maskT_t(j)
             for i, u in enumerate(preps(c)):
@@ -389,14 +397,14 @@ def tile_attention_gear_t_kernel(tc, q, k, v, start_pos, seqlen, mask, out):
                 prep_evac(u[0], u[1], "act")
             if ok(c - 2):
                 evac_e(c - 2, False)
-            if ok(c - 4):
-                o_evac(c - 4, c % 2 == 1)
-                store(c - 4)
-            if ok(c - 1):
-                e_t(c - 1, 0)
-                e_t(c - 1, 1)
+            if ok(c - 4) and not both_on_vector(c - 4):
+                o_evac(c - 4, 0, False)
             for j in MASKS.get(c, []):
                 maskT_evac(j)
+            if ok(c - 1):
+                for hh in range(H):
+                    for u in range(U):
+                        e_t(c - 1, hh, u)
             xb, xr = divmod(c + 2, NT)
             if 0 <= xb < B:
                 regroup_v(xb, xr)
@@ -452,45 +460,47 @@ def tile_attention_gear_t_kernel(tc, q, k, v, start_pos, seqlen, mask, out):
             ob = work.tile([P, D], F32, tag="zob", name="zob", bufs=2)
             po = st[("zpo", hh)]
             sc = st[("rc", z)][:, hh:hh + 1]
-            if on_vector:
-                nc.vector.tensor_scalar(out=ob[:], in0=po[:], scalar1=sc, scalar2=None, op0=ALU.mult)
-            else:
-                nc.scalar.activation(out=ob[:], in_=po[:], func=ACTF.Copy, scale=sc)
+            scaled_copy(on_vector, ob[:], po[:], sc)
             nc.sync.dma_start(out=out[zb].rearrange("(p j) h d -> p j h d", j=NT)[:, NT - 1, hh, :], in_=ob[:])
 
-        e_t(z - 1, 0)
-        e_t(z - 1, 1)
+        for hh in range(H):
+            for u in range(U):
+                e_t(z - 1, hh, u)
+        o_evac(z - 5, 1, True)
+        store(z - 5)
         quant_v(zb, NT - 1)
-        recip(z - 3)
+        recip((z - 3) // 2)
         quant_e(z - 3)
         pv(z - 4)
         expo(z, 0)
         evac_e(z - 2, False)
         expo(z, 1)
         z_e_t(0)
-        o_evac(z - 4, True)
+        o_evac(z - 4, 0, True)
+        o_evac(z - 4, 1, True)
         store(z - 4)
-        pv(z - 3)
         z_evac(0, True)
         z_e_t(1)
+        pv(z - 3)
         evac_e(z - 1, False)
         z_evac(1, False)
-        recip(z - 2)
         quant_e(z - 2)
         z_quant(0)
-        recip(z)
+        recip(z // 2)
         z_quant(1)
         pv(z - 2)
         z_pv(0)
         z_pv(1)
-        o_evac(z - 3, False)
+        o_evac(z - 3, 0, False)
+        o_evac(z - 3, 1, False)
         store(z - 3)
-        recip(z - 1)
         quant_e(z - 1)
         pv(z - 1)
-        o_evac(z - 2, True)
+        o_evac(z - 2, 0, True)
+        o_evac(z - 2, 1, True)
         store(z - 2)
         z_out(1, False)
         z_out(0, True)
-        o_evac(z - 1, False)
+        o_evac(z - 1, 0, False)
+        o_evac(z - 1, 1, True)
         store(z - 1)

@@ -152,12 +152,21 @@ def tile_attention_gear_t_kernel(tc, q, k, v, start_pos, seqlen, mask, out):
         def maskT_evac(j):
             mb = work.tile([P, NT, P], BF16, tag="mb", name="mb", bufs=2)
             nc.vector.tensor_copy(out=mb[:], in_=st[("pm", j)][:])
+            st[("mb", j)] = mb
+
+        def maskT_wide(j):
             nc.gpsimd.tensor_scalar(
-                out=maskT[:, j, :, :], in0=mb[:], scalar1=16.0, scalar2=0.0, op0=ALU.mult, op1=ALU.add
+                out=maskT[:, j, :, :], in0=st[("mb", j)][:], scalar1=16.0, scalar2=0.0, op0=ALU.mult, op1=ALU.add
             )
 
+        def mmask(n, hh):
+            return hh == 0 and n < 12
+
+        def tmask(n, hh):
+            return not mmask(n, hh) and (hh == 0 or (n >= 8 and n % 8 == 4))
+
         def pe_mask(n, hh):
-            return hh == 0 or (n >= 8 and n % 8 == 4)
+            return mmask(n, hh) or tmask(n, hh)
 
         def qk_pass(n, hh, e):
             b, j = divmod(n, NT)
@@ -171,7 +180,7 @@ def tile_attention_gear_t_kernel(tc, q, k, v, start_pos, seqlen, mask, out):
                 start=(e == 0),
                 stop=(e == 1 and not pe_mask(n, hh)),
             )
-            if e == 1 and hh == 0 and n < NMM:
+            if e == 1 and mmask(n, hh):
                 nc.tensor.matmul(out=ps[:], lhsT=ident16[:], rhs=mask_sb[:, j, :], start=False, stop=True)
 
         def qk(n, hh):
@@ -346,20 +355,20 @@ def tile_attention_gear_t_kernel(tc, q, k, v, start_pos, seqlen, mask, out):
                 return [(b1, r)]
             return []
 
-        def both_on_vector(n):
-            return n >= 6 and n % 8 == 6
+        def o_vec(n, hh):
+            return hh == 1 or (n >= 6 and n % 8 == 6)
 
-        MASKS = {1: [0], 2: [1, 2], 3: [3]}
+        MASKS = {0: [0], 1: [1], 2: [2], 3: [3]}
         for c in range(-1, NS - 1):
             if ok(c + 1):
                 score(c + 1, 0)
                 score(c + 1, 1)
             if ok(c - 5):
-                if both_on_vector(c - 5):
-                    o_evac(c - 5, 0, True)
-                o_evac(c - 5, 1, True)
+                for hh in range(H):
+                    if o_vec(c - 5, hh):
+                        o_evac(c - 5, hh, True)
                 store(c - 5)
-            if c + 1 == NS - 1:
+            if c + 1 == NS - 1 and not pe_mask(c + 1, 1):
                 rowmin(c + 1, 1)
             if ok(c - 3):
                 if c % 2 == 1:
@@ -368,6 +377,8 @@ def tile_attention_gear_t_kernel(tc, q, k, v, start_pos, seqlen, mask, out):
             vb, vr = divmod(c, NT)
             if c > 0:
                 quant_v(vb, vr)
+            for j in MASKS.get(c - 1, []):
+                maskT_evac(j)
             if c + 1 < NS - 1 and not pe_mask(c + 1, 1):
                 rowmin(c + 1, 1)
             if c == 0:
@@ -381,7 +392,7 @@ def tile_attention_gear_t_kernel(tc, q, k, v, start_pos, seqlen, mask, out):
                 qk(c + 2, 1)
             if scores:
                 for hh in range(H):
-                    if pe_mask(c + 2, hh) and (hh == 1 or c + 2 >= NMM):
+                    if tmask(c + 2, hh):
                         add_mask(c + 2, hh)
             for j in MASKS.get(c, []):
                 maskT_t(j)
@@ -397,10 +408,10 @@ def tile_attention_gear_t_kernel(tc, q, k, v, start_pos, seqlen, mask, out):
                 prep_evac(u[0], u[1], "act")
             if ok(c - 2):
                 evac_e(c - 2, False)
-            if ok(c - 4) and not both_on_vector(c - 4):
-                o_evac(c - 4, 0, False)
-            for j in MASKS.get(c, []):
-                maskT_evac(j)
+            if ok(c - 4):
+                for hh in range(H):
+                    if not o_vec(c - 4, hh):
+                        o_evac(c - 4, hh, False)
             if ok(c - 1):
                 for hh in range(H):
                     for u in range(U):
@@ -408,6 +419,8 @@ def tile_attention_gear_t_kernel(tc, q, k, v, start_pos, seqlen, mask, out):
             xb, xr = divmod(c + 2, NT)
             if 0 <= xb < B:
                 regroup_v(xb, xr)
+            for j in MASKS.get(c - 1, []):
+                maskT_wide(j)
             nb, cr = divmod(c + 11, NT)
             if c >= 1 and cr == 0 and nb < B:
                 load_kq(nb)
@@ -466,7 +479,9 @@ def tile_attention_gear_t_kernel(tc, q, k, v, start_pos, seqlen, mask, out):
         for hh in range(H):
             for u in range(U):
                 e_t(z - 1, hh, u)
-        o_evac(z - 5, 1, True)
+        for hh in range(H):
+            if o_vec(z - 5, hh):
+                o_evac(z - 5, hh, True)
         store(z - 5)
         quant_v(zb, NT - 1)
         recip((z - 3) // 2)

@@ -163,7 +163,7 @@ def tile_attention_gear_t_kernel(tc, q, k, v, start_pos, seqlen, mask, out):
             return hh == 0 and n < 12
 
         def tmask(n, hh):
-            return not mmask(n, hh) and (hh == 0 or (n >= 8 and n % 8 == 4))
+            return not mmask(n, hh) and (hh == 0 or (n >= 8 and n % 4 == 0) or n >= 27)
 
         def pe_mask(n, hh):
             return mmask(n, hh) or tmask(n, hh)
@@ -356,7 +356,7 @@ def tile_attention_gear_t_kernel(tc, q, k, v, start_pos, seqlen, mask, out):
             return []
 
         def o_vec(n, hh):
-            return hh == 1 or (n >= 6 and n % 8 == 6)
+            return hh == 1 or (n >= 6 and n % 4 == 2)
 
         MASKS = {0: [0], 1: [1], 2: [2], 3: [3]}
         for c in range(-1, NS - 1):

@@ -19,6 +19,7 @@ NS = B * NT
 FLOPS = 2 * (2 * B * H * S * S * D)
 
 NMM = 12
+NWARM = 14
 U = 2
 
 
@@ -90,11 +91,30 @@ def tile_attention_gear_t_kernel(tc, q, k, v, start_pos, seqlen, mask, out):
 
         UNITS = [("k", 0), ("q", 0), ("k", 1), ("q", 1)]
 
-        qT0 = [tp.tile([P, 2, S], BF16, tag="qT%d" % hh, name="qT0") for hh in range(H)]
-        kT0 = [tp.tile([P, 2, S], BF16, tag="kT%d" % hh, name="kT0") for hh in range(H)]
-        for hh in range(H):
-            st[("qT", 0, hh)] = qT0[hh][:].rearrange("p e s -> p s e")
-            st[("kT", 0, hh)] = kT0[hh][:].rearrange("p e s -> p s e")
+        ones = const.tile([P, S], BF16, name="ones", align_bytes=64)
+        nc.vector.memset(ones[:], 1.0)
+        ones_c = const.tile([P, P], U32, name="ones_c", align_bytes=64)
+        ones_s = const.tile([P, P], U8, name="ones_s", align_bytes=64)
+        nc.vector.quantize_mx(out=ones_c[:].bitcast(FP8X4), scales=ones_s[:], in_=ones[:])
+
+        def warm_up(n):
+            pw = ps_e.tile([P, P], F32, tag="pe", name="pw")
+            for i in range(n):
+                nc.tensor.matmul_mx(
+                    out=pw[:],
+                    lhsT=ones_c[:].bitcast(FP8X4),
+                    lhsT_scale=ones_s[:],
+                    rhs=ones_c[:].bitcast(FP8X4),
+                    rhs_scale=ones_s[:],
+                    start=True,
+                    stop=True,
+                )
+
+        warm_up(NWARM)
+
+        for which, h in UNITS:
+            st[("T0", which, h)] = tp.tile([P, S], F32, tag="%sT%d" % (which, h), name="dst0")
+            st[(which + "T", 0, h)] = st[("T0", which, h)][:].bitcast(BF16).rearrange("p (s e) -> p s e", e=2)
 
         def copy_out(on_vector, dst, src):
             if on_vector:
@@ -102,23 +122,16 @@ def tile_attention_gear_t_kernel(tc, q, k, v, start_pos, seqlen, mask, out):
             else:
                 nc.scalar.copy(out=dst, in_=src)
 
-        def k0_part(hh, e, pool, tag, on_vector):
-            pt = pool.tile([P, S], BF16, tag=tag, name="ptk")
-            for i in range(NT):
-                cs = slice(hh * D + e * P, hh * D + (e + 1) * P)
-                nc.tensor.transpose(out=pt[:, i * P:(i + 1) * P], in_=k_raw0[:, i, cs], identity=ident_b[:])
-            copy_out(on_vector, kT0[hh][:, e, :], pt[:])
-
-        def q0_part(hh, j0, j1, pool, tag, on_vector):
-            pt = pool.tile([P, 2, (j1 - j0) * P], BF16, tag=tag, name="ptq")
-            for j in range(j0, j1):
-                for e in range(2):
-                    nc.tensor.transpose(
-                        out=pt[:, e, (j - j0) * P:(j - j0 + 1) * P],
-                        in_=q_raw0[:, j, hh * D + e * P:hh * D + (e + 1) * P],
-                        identity=ident_b[:],
-                    )
-            copy_out(on_vector, qT0[hh][:, :, j0 * P:j1 * P], pt[:])
+        def part0(which, h, i0, i1, pool, tag, on_vector):
+            pt = pool.tile([P, (i1 - i0) * P], F32, tag=tag, name="pt0")
+            words = st[(which + "_raw", 0)][:].bitcast(F32)
+            for i in range(i0, i1):
+                nc.tensor.transpose(
+                    out=pt[:, (i - i0) * P:(i - i0 + 1) * P],
+                    in_=words[:, i, h * P:(h + 1) * P],
+                    identity=ident_f[:],
+                )
+            copy_out(on_vector, st[("T0", which, h)][:, i0 * P:i1 * P], pt[:])
 
         def prep_t(b, r, pool, tag):
             which, h = UNITS[r]
@@ -160,7 +173,7 @@ def tile_attention_gear_t_kernel(tc, q, k, v, start_pos, seqlen, mask, out):
             )
 
         def mmask(n, hh):
-            return hh == 0 and n < 12
+            return n == 0 or (hh == 0 and n < 11)
 
         def tmask(n, hh):
             return not mmask(n, hh) and (hh == 0 or (n >= 8 and n % 4 == 0) or n >= 27)
@@ -302,9 +315,9 @@ def tile_attention_gear_t_kernel(tc, q, k, v, start_pos, seqlen, mask, out):
                 in_=st[("vgrp", b, r)][:].rearrange("p c t -> p (c t)"),
             )
 
-        def pv(n):
+        def pv(n, pool=ps_o, tag="po"):
             b, j = divmod(n, NT)
-            po = ps_o.tile([P, H, D], F32, tag="po", name="po")
+            po = pool.tile([P, H, D], F32, tag=tag, name="po")
             for hh in range(H):
                 nc.tensor.matmul_mx(
                     out=po[:, hh, :],
@@ -325,7 +338,7 @@ def tile_attention_gear_t_kernel(tc, q, k, v, start_pos, seqlen, mask, out):
 
         def o_evac(n, hh, on_vector):
             if ("ob", n) not in st:
-                st[("ob", n)] = work.tile([P, H, D], F32, tag="ob", name="ob", bufs=4)
+                st[("ob", n)] = work.tile([P, H, D], F32, tag="ob", name="ob", bufs=8)
             scaled_copy(on_vector, st[("ob", n)][:, hh, :], st[("po", n)][:, hh, :], st[("rc", n)][:, hh:hh + 1])
 
         def store(n):
@@ -335,16 +348,16 @@ def tile_attention_gear_t_kernel(tc, q, k, v, start_pos, seqlen, mask, out):
                 in_=st[("ob", n)][:].rearrange("p h d -> p (h d)"),
             )
 
-        q0_part(0, 0, 1, ps_t, "t", True)
-        k0_part(0, 0, ps_s, "s", False)
-        k0_part(0, 1, ps_s, "s", True)
-        q0_part(1, 0, 1, ps_o, "po", True)
-        k0_part(1, 0, ps_e, "pe", False)
-        k0_part(1, 1, ps_e, "pe", True)
+        part0("q", 0, 0, 1, ps_t, "t", True)
+        part0("k", 0, 0, 2, ps_s, "s", False)
+        part0("k", 0, 2, NT, ps_s, "s", True)
+        part0("q", 1, 0, 1, ps_o, "po", False)
+        part0("k", 1, 0, 2, ps_e, "pe", True)
+        part0("k", 1, 2, NT, ps_e, "pe", False)
         qk(0, 0)
-        q0_part(0, 1, NT, ps_t, "t", False)
+        part0("q", 0, 1, NT, ps_t, "t", True)
         qk(0, 1)
-        q0_part(1, 1, NT, ps_o, "po", False)
+        part0("q", 1, 1, NT, ps_o, "po", False)
         regroup_v(0, 0)
 
         def preps(c):
@@ -375,14 +388,14 @@ def tile_attention_gear_t_kernel(tc, q, k, v, start_pos, seqlen, mask, out):
                     recip((c - 3) // 2)
                 quant_e(c - 3)
             vb, vr = divmod(c, NT)
+            if c == 1:
+                quant_v(0, 0)
             if c > 0:
                 quant_v(vb, vr)
             for j in MASKS.get(c - 1, []):
                 maskT_evac(j)
             if c + 1 < NS - 1 and not pe_mask(c + 1, 1):
                 rowmin(c + 1, 1)
-            if c == 0:
-                quant_v(0, 0)
             scores = ok(c + 2)
             if scores:
                 qk(c + 2, 0)
@@ -479,43 +492,43 @@ def tile_attention_gear_t_kernel(tc, q, k, v, start_pos, seqlen, mask, out):
         for hh in range(H):
             for u in range(U):
                 e_t(z - 1, hh, u)
+        quant_v(zb, NT - 1)
         for hh in range(H):
             if o_vec(z - 5, hh):
                 o_evac(z - 5, hh, True)
         store(z - 5)
-        quant_v(zb, NT - 1)
         recip((z - 3) // 2)
         quant_e(z - 3)
-        pv(z - 4)
         expo(z, 0)
-        evac_e(z - 2, False)
         expo(z, 1)
+        pv(z - 4)
         z_e_t(0)
-        o_evac(z - 4, 0, True)
-        o_evac(z - 4, 1, True)
-        store(z - 4)
-        z_evac(0, True)
         z_e_t(1)
-        pv(z - 3)
+        evac_e(z - 2, False)
         evac_e(z - 1, False)
+        z_evac(0, False)
         z_evac(1, False)
+        pv(z - 3)
+        for hh in range(H):
+            o_evac(z - 4, hh, True)
+        store(z - 4)
+        recip(z // 2)
         quant_e(z - 2)
         z_quant(0)
-        recip(z // 2)
         z_quant(1)
-        pv(z - 2)
+        quant_e(z - 1)
+        for hh in range(H):
+            o_evac(z - 3, hh, False)
+        store(z - 3)
+        pv(z - 2, ps_t, "t")
         z_pv(0)
         z_pv(1)
-        o_evac(z - 3, 0, False)
-        o_evac(z - 3, 1, False)
-        store(z - 3)
-        quant_e(z - 1)
-        pv(z - 1)
-        o_evac(z - 2, 0, True)
-        o_evac(z - 2, 1, True)
+        pv(z - 1, ps_e, "pe")
+        for hh in range(H):
+            o_evac(z - 2, hh, True)
         store(z - 2)
-        z_out(1, False)
-        z_out(0, True)
-        o_evac(z - 1, 0, False)
-        o_evac(z - 1, 1, True)
+        z_out(0, False)
+        z_out(1, True)
+        for hh in range(H):
+            o_evac(z - 1, hh, hh == 1)
         store(z - 1)

@@ -71,8 +71,9 @@ def tile_attention_gear_t_kernel(tc, q, k, v, start_pos, seqlen, mask, out):
             if hh == 0:
                 nc.sync.dma_start(out=mask_sb[:, 0, :], in_=mask_pj[:, 0, :])
         nc.sync.dma_start(out=q_raw0[:, 1:, :], in_=q_pj[:, 1:, :])
-        nc.sync.dma_start(out=mask_sb[:, 1:, :], in_=mask_pj[:, 1:, :])
+        nc.sync.dma_start(out=mask_sb[:, 1, :], in_=mask_pj[:, 1, :])
         load_kq(1)
+        nc.sync.dma_start(out=mask_sb[:, 2:, :], in_=mask_pj[:, 2:, :])
         load_v(0)
         load_v(1)
         load_kq(2)
@@ -176,7 +177,7 @@ def tile_attention_gear_t_kernel(tc, q, k, v, start_pos, seqlen, mask, out):
             return n == 0 or (hh == 0 and n < 11)
 
         def tmask(n, hh):
-            return not mmask(n, hh) and (hh == 0 or (n >= 8 and n % 4 == 0) or n >= 27)
+            return not mmask(n, hh) and (hh == 0 or (8 <= n < 27 and n % 2 == 0) or n in (27, 28, 29, 30, 31))
 
         def pe_mask(n, hh):
             return mmask(n, hh) or tmask(n, hh)
@@ -245,15 +246,15 @@ def tile_attention_gear_t_kernel(tc, q, k, v, start_pos, seqlen, mask, out):
         def expo(n, hh):
             if hh == 0:
                 st[("e2", n)] = work.tile([P, H, S], BF16, tag="e2", name="e2")
-                if n % 2 == 0:
-                    st[("rs", n // 2)] = small.tile([P, 2, H], F32, tag="rs", name="rs", bufs=4)
+                if n % NT == 0:
+                    st[("rs", n // NT)] = small.tile([P, NT, H], F32, tag="rs", name="rs", bufs=4)
             nc.scalar.activation(
                 out=st[("e2", n)][:, hh, :].rearrange("p (u w e) -> p u w e", u=U, e=2),
                 in_=st[("s2", n)][:, hh, :].rearrange("p (w u e) -> p u w e", u=U, e=2),
                 func=ACTF.Exp,
                 bias=st[("negm", n)][:, hh:hh + 1],
                 scale=-1.0,
-                accum_out=st[("rs", n // 2)][:, n % 2, hh:hh + 1],
+                accum_out=st[("rs", n // NT)][:, n % NT, hh:hh + 1],
             )
 
         def e_t(n, hh, u):
@@ -286,10 +287,10 @@ def tile_attention_gear_t_kernel(tc, q, k, v, start_pos, seqlen, mask, out):
             st[("es", n)] = es
 
         def recip(m):
-            rc = small.tile([P, 2, H], F32, tag="rc", name="rc")
+            rc = small.tile([P, NT, H], F32, tag="rc", name="rc")
             nc.vector.reciprocal(out=rc[:], in_=st[("rs", m)][:])
-            st[("rc", 2 * m)] = rc[:, 0, :]
-            st[("rc", 2 * m + 1)] = rc[:, 1, :]
+            for i in range(NT):
+                st[("rc", NT * m + i)] = rc[:, i, :]
 
         def regroup_v(b, r):
             vg = work.tile([P, P, NT], BF16, tag="vgrp", name="vgrp", bufs=2, align_bytes=64)
@@ -369,9 +370,9 @@ def tile_attention_gear_t_kernel(tc, q, k, v, start_pos, seqlen, mask, out):
             return []
 
         def o_vec(n, hh):
-            return hh == 1 or (n >= 6 and n % 4 == 2)
+            return hh == 1 or (n >= 6 and n % 2 == 0)
 
-        MASKS = {0: [0], 1: [1], 2: [2], 3: [3]}
+        MASKS = {1: [0], 2: [1], 3: [2], 4: [3]}
         for c in range(-1, NS - 1):
             if ok(c + 1):
                 score(c + 1, 0)
@@ -384,8 +385,8 @@ def tile_attention_gear_t_kernel(tc, q, k, v, start_pos, seqlen, mask, out):
             if c + 1 == NS - 1 and not pe_mask(c + 1, 1):
                 rowmin(c + 1, 1)
             if ok(c - 3):
-                if c % 2 == 1:
-                    recip((c - 3) // 2)
+                if c % NT == 0:
+                    recip(c // NT - 1)
                 quant_e(c - 3)
             vb, vr = divmod(c, NT)
             if c == 1:
@@ -497,7 +498,6 @@ def tile_attention_gear_t_kernel(tc, q, k, v, start_pos, seqlen, mask, out):
             if o_vec(z - 5, hh):
                 o_evac(z - 5, hh, True)
         store(z - 5)
-        recip((z - 3) // 2)
         quant_e(z - 3)
         expo(z, 0)
         expo(z, 1)
@@ -512,7 +512,7 @@ def tile_attention_gear_t_kernel(tc, q, k, v, start_pos, seqlen, mask, out):
         for hh in range(H):
             o_evac(z - 4, hh, True)
         store(z - 4)
-        recip(z // 2)
+        recip(z // NT)
         quant_e(z - 2)
         z_quant(0)
         z_quant(1)

@@ -68,8 +68,7 @@ def tile_attention_gear_t_kernel(tc, q, k, v, start_pos, seqlen, mask, out):
             nc.sync.dma_start(out=q_raw0[:, 0, ds], in_=q_pj[:, 0, ds])
             for t in range(0, NT, 2):
                 nc.sync.dma_start(out=k_raw0[:, t:t + 2, ds], in_=k_tp[:, t:t + 2, ds])
-            if hh == 0:
-                nc.sync.dma_start(out=mask_sb[:, 0, :], in_=mask_pj[:, 0, :])
+        nc.sync.dma_start(out=mask_sb[:, 0, :], in_=mask_pj[:, 0, :])
         nc.sync.dma_start(out=q_raw0[:, 1:, :], in_=q_pj[:, 1:, :])
         nc.sync.dma_start(out=mask_sb[:, 1, :], in_=mask_pj[:, 1, :])
         load_kq(1)
@@ -174,10 +173,10 @@ def tile_attention_gear_t_kernel(tc, q, k, v, start_pos, seqlen, mask, out):
             )
 
         def mmask(n, hh):
-            return n == 0 or (hh == 0 and n < 11)
+            return n in (0, 2) or (hh == 0 and n < 10)
 
         def tmask(n, hh):
-            return not mmask(n, hh) and (hh == 0 or (8 <= n < 27 and n % 2 == 0) or n in (27, 28, 29, 30, 31))
+            return not mmask(n, hh) and (hh == 0 or (8 <= n < 27 and n % 2 == 0) or n >= 27)
 
         def pe_mask(n, hh):
             return mmask(n, hh) or tmask(n, hh)
@@ -370,7 +369,7 @@ def tile_attention_gear_t_kernel(tc, q, k, v, start_pos, seqlen, mask, out):
             return []
 
         def o_vec(n, hh):
-            return hh == 1 or (n >= 6 and n % 2 == 0)
+            return hh == 1 or (n >= 4 and n % 2 == 0)
 
         MASKS = {1: [0], 2: [1], 3: [2], 4: [3]}
         for c in range(-1, NS - 1):
@@ -504,19 +503,19 @@ def tile_attention_gear_t_kernel(tc, q, k, v, start_pos, seqlen, mask, out):
         pv(z - 4)
         z_e_t(0)
         z_e_t(1)
+        evac_e(z - 1, True)
         evac_e(z - 2, False)
-        evac_e(z - 1, False)
         z_evac(0, False)
         z_evac(1, False)
         pv(z - 3)
-        for hh in range(H):
-            o_evac(z - 4, hh, True)
-        store(z - 4)
         recip(z // NT)
         quant_e(z - 2)
         z_quant(0)
         z_quant(1)
         quant_e(z - 1)
+        for hh in range(H):
+            o_evac(z - 4, hh, False)
+        store(z - 4)
         for hh in range(H):
             o_evac(z - 3, hh, False)
         store(z - 3)

from contextlib import ExitStack

import concourse.mybir as mybir
from concourse.masks import make_identity

F32 = mybir.dt.float32
BF16 = mybir.dt.bfloat16
U32 = mybir.dt.uint32
U8 = mybir.dt.uint8
FP8X4 = mybir.dt.float8_e4m3fn_x4
ALU = mybir.AluOpType
ACTF = mybir.ActivationFunctionType
AX = mybir.AxisListType

B, S, H, D = 8, 512, 2, 256
P = 128
NT = S // P
NS = B * NT
FLOPS = 2 * (2 * B * H * S * S * D)

NMM = 12
NWARM = 14
U = 2


def tile_attention_gear_t_kernel(tc, q, k, v, start_pos, seqlen, mask, out):
    nc = tc.nc
    with ExitStack() as ctx:
        ctx.enter_context(tc.manual_schedule())
        const = ctx.enter_context(tc.tile_pool(name="const", bufs=1))
        raw = ctx.enter_context(tc.tile_pool(name="raw", bufs=2))
        tp = ctx.enter_context(tc.tile_pool(name="tp", bufs=2))
        work = ctx.enter_context(tc.tile_pool(name="work", bufs=3))
        small = ctx.enter_context(tc.tile_pool(name="small", bufs=4))
        ps_s = ctx.enter_context(tc.psum_pool(name="ps_s", bufs=3))
        ps_t = ctx.enter_context(tc.psum_pool(name="ps_t", bufs=1))
        ps_e = ctx.enter_context(tc.psum_pool(name="ps_e", bufs=2))
        ps_o = ctx.enter_context(tc.psum_pool(name="ps_o", bufs=2))

        st = {}

        def ok(n):
            return 0 <= n < NS

        def load_kq(b):
            k_raw = raw.tile([P, NT, H * D], BF16, tag="k_raw")
            nc.sync.dma_start(out=k_raw[:], in_=k[b].rearrange("(t p) h d -> p t (h d)", p=P))
            q_raw = raw.tile([P, NT, H * D], BF16, tag="q_raw")
            nc.sync.dma_start(out=q_raw[:], in_=q[b].rearrange("(p j) h d -> p j (h d)", j=NT))
            st[("k_raw", b)] = k_raw
            st[("q_raw", b)] = q_raw

        def load_v(b):
            v_raw = raw.tile([P, NT, H * D], BF16, tag="v_raw", bufs=4)
            nc.sync.dma_start(out=v_raw[:], in_=v[b].rearrange("(p t) h d -> p t (h d)", t=NT))
            st[("v_raw", b)] = v_raw

        k_raw0 = raw.tile([P, NT, H * D], BF16, tag="k_raw", name="k_raw0")
        q_raw0 = raw.tile([P, NT, H * D], BF16, tag="q_raw", name="q_raw0")
        st[("k_raw", 0)] = k_raw0
        st[("q_raw", 0)] = q_raw0
        mask_sb = const.tile([P, NT, S], BF16, name="mask_sb")
        mask_pj = mask[0, 0].rearrange("(p j) c -> p j c", j=NT)
        k_tp = k[0].rearrange("(t p) h d -> p t (h d)", p=P)
        q_pj = q[0].rearrange("(p j) h d -> p j (h d)", j=NT)
        for hh in range(H):
            ds = slice(hh * D, (hh + 1) * D)
            nc.sync.dma_start(out=q_raw0[:, 0, ds], in_=q_pj[:, 0, ds])
            for t in range(0, NT, 2):
                nc.sync.dma_start(out=k_raw0[:, t:t + 2, ds], in_=k_tp[:, t:t + 2, ds])
        nc.sync.dma_start(out=mask_sb[:, 0, :], in_=mask_pj[:, 0, :])
        nc.sync.dma_start(out=q_raw0[:, 1:, :], in_=q_pj[:, 1:, :])
        nc.sync.dma_start(out=mask_sb[:, 1, :], in_=mask_pj[:, 1, :])
        load_kq(1)
        nc.sync.dma_start(out=mask_sb[:, 2:, :], in_=mask_pj[:, 2:, :])
        load_v(0)
        load_v(1)
        load_kq(2)
        load_v(2)

        ident_b = const.tile([P, P], BF16, name="ident_b")
        make_identity(nc, ident_b[:])
        ident_f = const.tile([P, P], F32, name="ident_f")
        make_identity(nc, ident_f[:])
        ident16 = const.tile([P, P], BF16, name="ident16")
        nc.gpsimd.tensor_scalar(out=ident16[:], in0=ident_b[:], scalar1=16.0, scalar2=0.0, op0=ALU.mult, op1=ALU.add)
        maskT = const.tile([P, NT, NT, P], F32, name="maskT")
        warm = const.tile([P, 1], F32, name="warm")
        nc.gpsimd.memset(warm[:], 0.0)
        nc.scalar.activation(out=warm[:], in_=warm[:], func=ACTF.Exp)

        UNITS = [("k", 0), ("q", 0), ("k", 1), ("q", 1)]

        ones = const.tile([P, S], BF16, name="ones", align_bytes=64)
        nc.vector.memset(ones[:], 1.0)
        ones_c = const.tile([P, P], U32, name="ones_c", align_bytes=64)
        ones_s = const.tile([P, P], U8, name="ones_s", align_bytes=64)
        nc.vector.quantize_mx(out=ones_c[:].bitcast(FP8X4), scales=ones_s[:], in_=ones[:])

        def warm_up(n):
            pw = ps_e.tile([P, P], F32, tag="pe", name="pw")
            for i in range(n):
                nc.tensor.matmul_mx(
                    out=pw[:],
                    lhsT=ones_c[:].bitcast(FP8X4),
                    lhsT_scale=ones_s[:],
                    rhs=ones_c[:].bitcast(FP8X4),
                    rhs_scale=ones_s[:],
                    start=True,
                    stop=True,
                )

        warm_up(NWARM)

        for which, h in UNITS:
            st[("T0", which, h)] = tp.tile([P, S], F32, tag="%sT%d" % (which, h), name="dst0")
            st[(which + "T", 0, h)] = st[("T0", which, h)][:].bitcast(BF16).rearrange("p (s e) -> p s e", e=2)

        def copy_out(on_vector, dst, src):
            if on_vector:
                nc.vector.tensor_copy(out=dst, in_=src)
            else:
                nc.scalar.copy(out=dst, in_=src)

        def part0(which, h, i0, i1, pool, tag, on_vector):
            pt = pool.tile([P, (i1 - i0) * P], F32, tag=tag, name="pt0")
            words = st[(which + "_raw", 0)][:].bitcast(F32)
            for i in range(i0, i1):
                nc.tensor.transpose(
                    out=pt[:, (i - i0) * P:(i - i0 + 1) * P],
                    in_=words[:, i, h * P:(h + 1) * P],
                    identity=ident_f[:],
                )
            copy_out(on_vector, st[("T0", which, h)][:, i0 * P:i1 * P], pt[:])

        def prep_t(b, r, pool, tag):
            which, h = UNITS[r]
            pt = pool.tile([P, S], F32, tag=tag, name="pt")
            words = st[(which + "_raw", b)][:].bitcast(F32)
            for i in range(NT):
                nc.tensor.transpose(
                    out=pt[:, i * P:(i + 1) * P],
                    in_=words[:, i, h * P:(h + 1) * P],
                    identity=ident_f[:],
                )
            st[("pt", b, r)] = pt

        def prep_evac(b, r, eng):
            which, h = UNITS[r]
            tag = "%sT%d" % (which, h)
            dst = tp.tile([P, S], F32, tag=tag, name="dstT")
            pt = st[("pt", b, r)]
            if eng == "act":
                nc.scalar.copy(out=dst[:], in_=pt[:])
            else:
                nc.vector.tensor_copy(out=dst[:], in_=pt[:])
            st[(which + "T", b, h)] = dst[:].bitcast(BF16).rearrange("p (s e) -> p s e", e=2)

        def maskT_t(j):
            pm = ps_o.tile([P, NT, P], BF16, tag="po", name="pm")
            for t in range(NT):
                nc.tensor.transpose(out=pm[:, t, :], in_=mask_sb[:, j, t * P:(t + 1) * P], identity=ident_b[:])
            st[("pm", j)] = pm

        def maskT_evac(j):
            mb = work.tile([P, NT, P], BF16, tag="mb", name="mb", bufs=2)
            nc.vector.tensor_copy(out=mb[:], in_=st[("pm", j)][:])
            st[("mb", j)] = mb

        def maskT_wide(j):
            nc.gpsimd.tensor_scalar(
                out=maskT[:, j, :, :], in0=st[("mb", j)][:], scalar1=16.0, scalar2=0.0, op0=ALU.mult, op1=ALU.add
            )

        def mmask(n, hh):
            return n in (0, 2) or (hh == 0 and n < 10)

        def tmask(n, hh):
            return not mmask(n, hh) and (hh == 0 or (8 <= n < 27 and n % 2 == 0) or n >= 27)

        def pe_mask(n, hh):
            return mmask(n, hh) or tmask(n, hh)

        def qk_pass(n, hh, e):
            b, j = divmod(n, NT)
            if e == 0:
                st[("ps", n, hh)] = ps_s.tile([P, S], F32, tag="s", name="ps")
            ps = st[("ps", n, hh)]
            nc.tensor.matmul(
                out=ps[:],
                lhsT=st[("qT", b, hh)][:, j * P:(j + 1) * P, e],
                rhs=st[("kT", b, hh)][:, :, e],
                start=(e == 0),
                stop=(e == 1 and not pe_mask(n, hh)),
            )
            if e == 1 and mmask(n, hh):
                nc.tensor.matmul(out=ps[:], lhsT=ident16[:], rhs=mask_sb[:, j, :], start=False, stop=True)

        def qk(n, hh):
            qk_pass(n, hh, 0)
            qk_pass(n, hh, 1)

        def add_mask(n, hh):
            b, j = divmod(n, NT)
            for t in range(NT):
                nc.tensor.matmul(
                    out=st[("ps", n, hh)][:, t * P:(t + 1) * P],
                    lhsT=maskT[:, j, t, :],
                    rhs=ident_f[:],
                    is_transpose=True,
                    start=False,
                    stop=(t == NT - 1),
                )

        def score(n, hh):
            b, j = divmod(n, NT)
            if hh == 0:
                st[("s2", n)] = work.tile([P, H, S], F32, tag="s2", name="s2")
                st[("negm", n)] = small.tile([P, H], F32, tag="negm", name="negm")
            if pe_mask(n, hh):
                nc.vector.tensor_scalar(
                    out=st[("s2", n)][:, hh, :],
                    in0=st[("ps", n, hh)][:],
                    scalar1=-1.0 / 16.0,
                    scalar2=None,
                    op0=ALU.mult,
                    op1=ALU.min,
                    accum_out=st[("negm", n)][:, hh:hh + 1],
                )
            else:
                nc.vector.scalar_tensor_tensor(
                    out=st[("s2", n)][:, hh, :],
                    in0=st[("ps", n, hh)][:],
                    scalar=-1.0 / 16.0,
                    in1=mask_sb[:, j, :],
                    op0=ALU.mult,
                    op1=ALU.subtract,
                )

        def rowmin(n, hh):
            nc.vector.tensor_reduce(
                out=st[("negm", n)][:, hh:hh + 1], in_=st[("s2", n)][:, hh, :], axis=AX.X, op=ALU.min
            )

        def expo(n, hh):
            if hh == 0:
                st[("e2", n)] = work.tile([P, H, S], BF16, tag="e2", name="e2")
                if n % NT == 0:
                    st[("rs", n // NT)] = small.tile([P, NT, H], F32, tag="rs", name="rs", bufs=4)
            nc.scalar.activation(
                out=st[("e2", n)][:, hh, :].rearrange("p (u w e) -> p u w e", u=U, e=2),
                in_=st[("s2", n)][:, hh, :].rearrange("p (w u e) -> p u w e", u=U, e=2),
                func=ACTF.Exp,
                bias=st[("negm", n)][:, hh:hh + 1],
                scale=-1.0,
                accum_out=st[("rs", n // NT)][:, n % NT, hh:hh + 1],
            )

        def e_t(n, hh, u):
            if hh == 0 and u == 0:
                st[("pe", n)] = ps_e.tile([P, U, H, P], F32, tag="pe", name="pe")
            nc.tensor.transpose(
                out=st[("pe", n)][:, u, hh, :],
                in_=st[("e2", n)][:].bitcast(F32)[:, hh, u * P:(u + 1) * P],
                identity=ident_f[:],
            )

        def evac_e(n, on_vector):
            grp = work.tile([P, H * P, NT], BF16, tag="grp", name="grp", align_bytes=64)
            src = st[("pe", n)][:].rearrange("p u h c -> p (h c) u")
            if on_vector:
                nc.vector.tensor_copy(out=grp[:].bitcast(F32), in_=src)
            else:
                nc.scalar.copy(out=grp[:].bitcast(F32), in_=src)
            st[("grp", n)] = grp

        def quant_e(n):
            ec = work.tile([P, H * P], U32, tag="ec", name="ec", align_bytes=64)
            es = work.tile([P, H * P], U8, tag="es", name="es", align_bytes=64)
            nc.vector.quantize_mx(
                out=ec[:].bitcast(FP8X4),
                scales=es[:],
                in_=st[("grp", n)][:].rearrange("p c t -> p (c t)"),
            )
            st[("ec", n)] = ec
            st[("es", n)] = es

        def recip(m):
            rc = small.tile([P, NT, H], F32, tag="rc", name="rc")
            nc.vector.reciprocal(out=rc[:], in_=st[("rs", m)][:])
            for i in range(NT):
                st[("rc", NT * m + i)] = rc[:, i, :]

        def regroup_v(b, r):
            vg = work.tile([P, P, NT], BF16, tag="vgrp", name="vgrp", bufs=2, align_bytes=64)
            st[("vgrp", b, r)] = vg
            cs = slice(r * P, (r + 1) * P)
            nc.gpsimd.tensor_scalar(
                out=vg[:],
                in0=st[("v_raw", b)][:, :, cs].rearrange("p t c -> p c t"),
                scalar1=1.0,
                scalar2=0.0,
                op0=ALU.mult,
                op1=ALU.add,
            )

        def quant_v(b, r):
            if r == 0:
                st[("vc", b)] = work.tile([P, H * D], U32, tag="vc", name="vc", align_bytes=64)
                st[("vs", b)] = work.tile([P, H * D], U8, tag="vs", name="vs", align_bytes=64)
            cs = slice(r * P, (r + 1) * P)
            nc.vector.quantize_mx(
                out=st[("vc", b)][:, cs].bitcast(FP8X4),
                scales=st[("vs", b)][:, cs],
                in_=st[("vgrp", b, r)][:].rearrange("p c t -> p (c t)"),
            )

        def pv(n, pool=ps_o, tag="po"):
            b, j = divmod(n, NT)
            po = pool.tile([P, H, D], F32, tag=tag, name="po")
            for hh in range(H):
                nc.tensor.matmul_mx(
                    out=po[:, hh, :],
                    lhsT=st[("ec", n)][:, hh * P:(hh + 1) * P].bitcast(FP8X4),
                    lhsT_scale=st[("es", n)][:, hh * P:(hh + 1) * P],
                    rhs=st[("vc", b)][:, hh * D:(hh + 1) * D].bitcast(FP8X4),
                    rhs_scale=st[("vs", b)][:, hh * D:(hh + 1) * D],
                    start=True,
                    stop=True,
                )
            st[("po", n)] = po

        def scaled_copy(on_vector, dst, src, sc):
            if on_vector:
                nc.vector.tensor_scalar(out=dst, in0=src, scalar1=sc, scalar2=None, op0=ALU.mult)
            else:
                nc.scalar.activation(out=dst, in_=src, func=ACTF.Copy, scale=sc)

        def o_evac(n, hh, on_vector):
            if ("ob", n) not in st:
                st[("ob", n)] = work.tile([P, H, D], F32, tag="ob", name="ob", bufs=8)
            scaled_copy(on_vector, st[("ob", n)][:, hh, :], st[("po", n)][:, hh, :], st[("rc", n)][:, hh:hh + 1])

        def store(n):
            b, j = divmod(n, NT)
            nc.sync.dma_start(
                out=out[b].rearrange("(p j) h d -> p j (h d)", j=NT)[:, j, :],
                in_=st[("ob", n)][:].rearrange("p h d -> p (h d)"),
            )

        part0("q", 0, 0, 1, ps_t, "t", True)
        part0("k", 0, 0, 2, ps_s, "s", False)
        part0("k", 0, 2, NT, ps_s, "s", True)
        part0("q", 1, 0, 1, ps_o, "po", False)
        part0("k", 1, 0, 2, ps_e, "pe", True)
        part0("k", 1, 2, NT, ps_e, "pe", False)
        qk(0, 0)
        part0("q", 0, 1, NT, ps_t, "t", True)
        qk(0, 1)
        part0("q", 1, 1, NT, ps_o, "po", False)
        regroup_v(0, 0)

        def preps(c):
            if c in (-1, 0):
                return [(1, 2 * (c + 1)), (1, 2 * (c + 1) + 1)]
            b1, r = divmod(c + 7, 4)
            if c >= 1 and b1 < B:
                return [(b1, r)]
            return []

        def o_vec(n, hh):
            return hh == 1 or (n >= 4 and n % 2 == 0)

        MASKS = {1: [0], 2: [1], 3: [2], 4: [3]}
        for c in range(-1, NS - 1):
            if ok(c + 1):
                score(c + 1, 0)
                score(c + 1, 1)
            if ok(c - 5):
                for hh in range(H):
                    if o_vec(c - 5, hh):
                        o_evac(c - 5, hh, True)
                store(c - 5)
            if c + 1 == NS - 1 and not pe_mask(c + 1, 1):
                rowmin(c + 1, 1)
            if ok(c - 3):
                if c % NT == 0:
                    recip(c // NT - 1)
                quant_e(c - 3)
            vb, vr = divmod(c, NT)
            if c == 1:
                quant_v(0, 0)
            if c > 0:
                quant_v(vb, vr)
            for j in MASKS.get(c - 1, []):
                maskT_evac(j)
            if c + 1 < NS - 1 and not pe_mask(c + 1, 1):
                rowmin(c + 1, 1)
            scores = ok(c + 2)
            if scores:
                qk(c + 2, 0)
            if ok(c - 4):
                pv(c - 4)
            if scores:
                qk(c + 2, 1)
            if scores:
                for hh in range(H):
                    if tmask(c + 2, hh):
                        add_mask(c + 2, hh)
            for j in MASKS.get(c, []):
                maskT_t(j)
            for i, u in enumerate(preps(c)):
                if i == 0:
                    prep_t(u[0], u[1], ps_t, "t")
                else:
                    prep_t(u[0], u[1], ps_o, "po")
            if ok(c):
                expo(c, 0)
                expo(c, 1)
            for u in preps(c - 1):
                prep_evac(u[0], u[1], "act")
            if ok(c - 2):
                evac_e(c - 2, False)
            if ok(c - 4):
                for hh in range(H):
                    if not o_vec(c - 4, hh):
                        o_evac(c - 4, hh, False)
            if ok(c - 1):
                for hh in range(H):
                    for u in range(U):
                        e_t(c - 1, hh, u)
            xb, xr = divmod(c + 2, NT)
            if 0 <= xb < B:
                regroup_v(xb, xr)
            for j in MASKS.get(c - 1, []):
                maskT_wide(j)
            nb, cr = divmod(c + 11, NT)
            if c >= 1 and cr == 0 and nb < B:
                load_kq(nb)
                load_v(nb)

        z = NS - 1
        zb = B - 1

        def z_e_t(hh):
            pe = ps_s.tile([P, U, P], F32, tag="s", name="zpe")
            words = st[("e2", z)][:].bitcast(F32)
            for u in range(U):
                nc.tensor.transpose(out=pe[:, u, :], in_=words[:, hh, u * P:(u + 1) * P], identity=ident_f[:])
            st[("zpe", hh)] = pe

        def z_evac(hh, on_vector):
            grp = work.tile([P, P, NT], BF16, tag="zgrp", name="zgrp", bufs=2, align_bytes=64)
            src = st[("zpe", hh)][:].rearrange("p u c -> p c u")
            if on_vector:
                nc.vector.tensor_copy(out=grp[:].bitcast(F32), in_=src)
            else:
                nc.scalar.copy(out=grp[:].bitcast(F32), in_=src)
            st[("zgrp", hh)] = grp

        def z_quant(hh):
            ec = work.tile([P, P], U32, tag="zec", name="zec", bufs=2, align_bytes=64)
            es = work.tile([P, P], U8, tag="zes", name="zes", bufs=2, align_bytes=64)
            nc.vector.quantize_mx(
                out=ec[:].bitcast(FP8X4),
                scales=es[:],
                in_=st[("zgrp", hh)][:].rearrange("p c t -> p (c t)"),
            )
            st[("zec", hh)] = ec
            st[("zes", hh)] = es

        def z_pv(hh):
            po = ps_s.tile([P, D], F32, tag="s", name="zpo")
            nc.tensor.matmul_mx(
                out=po[:],
                lhsT=st[("zec", hh)][:].bitcast(FP8X4),
                lhsT_scale=st[("zes", hh)][:],
                rhs=st[("vc", zb)][:, hh * D:(hh + 1) * D].bitcast(FP8X4),
                rhs_scale=st[("vs", zb)][:, hh * D:(hh + 1) * D],
                start=True,
                stop=True,
            )
            st[("zpo", hh)] = po

        def z_out(hh, on_vector):
            ob = work.tile([P, D], F32, tag="zob", name="zob", bufs=2)
            po = st[("zpo", hh)]
            sc = st[("rc", z)][:, hh:hh + 1]
            scaled_copy(on_vector, ob[:], po[:], sc)
            nc.sync.dma_start(out=out[zb].rearrange("(p j) h d -> p j h d", j=NT)[:, NT - 1, hh, :], in_=ob[:])

        for hh in range(H):
            for u in range(U):
                e_t(z - 1, hh, u)
        quant_v(zb, NT - 1)
        for hh in range(H):
            if o_vec(z - 5, hh):
                o_evac(z - 5, hh, True)
        store(z - 5)
        quant_e(z - 3)
        expo(z, 0)
        expo(z, 1)
        pv(z - 4)
        z_e_t(0)
        z_e_t(1)
        evac_e(z - 1, True)
        evac_e(z - 2, False)
        z_evac(0, False)
        z_evac(1, False)
        pv(z - 3)
        recip(z // NT)
        quant_e(z - 2)
        z_quant(0)
        z_quant(1)
        quant_e(z - 1)
        for hh in range(H):
            o_evac(z - 4, hh, False)
        store(z - 4)
        for hh in range(H):
            o_evac(z - 3, hh, False)
        store(z - 3)
        pv(z - 2, ps_t, "t")
        z_pv(0)
        z_pv(1)
        pv(z - 1, ps_e, "pe")
        for hh in range(H):
            o_evac(z - 2, hh, True)
        store(z - 2)
        z_out(0, False)
        z_out(1, True)
        for hh in range(H):
            o_evac(z - 1, hh, hh == 1)
        store(z - 1)
